import numpy as np
import ml_dtypes


def mxq(x, axis, fmt="e4m3"):
    dtype, down = {"e4m3": (ml_dtypes.float8_e4m3fn, 7), "e5m2": (ml_dtypes.float8_e5m2, 14)}[fmt]
    v = np.moveaxis(np.asarray(x, np.float32).astype(ml_dtypes.bfloat16).astype(np.float64), axis, -1)
    blocks = v.reshape(v.shape[:-1] + (-1, 32))
    amax = np.abs(blocks).max(-1, keepdims=True)
    byte = np.maximum(np.where(amax > 0, np.frexp(amax)[1] - 1 + 127, 0) - down, 1)
    scale = np.exp2(byte - 127.0)
    codes = (blocks / scale).astype(np.float32).astype(dtype).astype(np.float64)
    return np.moveaxis((codes * scale).reshape(v.shape), -1, axis)


WIDE = False


def mx_kscale(k):
    if not WIDE:
        return np.ones(k)
    levels = np.array([10, -10, 5, -5, 0])
    a = np.random.permutation(np.resize(levels, k // 512 * 4)).reshape(k // 512, 4)
    idx = np.arange(k)
    return np.exp2(a[idx // 512, idx % 128 // 32])


BF16 = ml_dtypes.bfloat16


def bf(x):
    return np.asarray(x, np.float32).astype(BF16)


def f64(x):
    return np.asarray(x).astype(np.float64)


LQ, LK, D, H, DK, DV = 1024, 1024, 2048, 4, 128, 128
HV = H * DV
LN_EPS = 1e-5


def setup_inputs():
    s = mx_kscale(HV)
    return {"attn_out": bf(np.random.standard_normal((H, LQ, DV)) * 0.7 * s.reshape(H, DV)[:, None, :]),
            "residual": bf(np.random.standard_normal((LQ, D))),
            "proj_w": bf(np.random.standard_normal((HV, D)) / np.sqrt(HV) / s[:, None]),
            "proj_b": bf(np.random.standard_normal(D) * 0.3),
            "ln_g": bf(1.0 + 0.1 * np.random.standard_normal(D)),
            "ln_b": bf(0.1 * np.random.standard_normal(D))}


def reference(attn_out, residual, proj_w, proj_b, ln_g, ln_b):
    x = f64(attn_out).transpose(1, 0, 2).reshape(LQ, HV)
    y = (mxq(x, 1, "e4m3") @ mxq(f64(proj_w), 0, "e4m3")) + f64(proj_b) + f64(residual)
    mu = y.mean(-1, keepdims=True)
    var = ((y - mu) ** 2).mean(-1, keepdims=True)
    return (y - mu) / np.sqrt(var + LN_EPS) * f64(ln_g) + f64(ln_b)

@@ -1,0 +1,133 @@
+from contextlib import ExitStack
+
+import concourse.mybir as mybir
+from concourse.masks import make_identity
+
+F32 = mybir.dt.float32
+BF16 = mybir.dt.bfloat16
+U32 = mybir.dt.uint32
+U8 = mybir.dt.uint8
+FP8X4 = mybir.dt.float8_e4m3fn_x4
+ALU = mybir.AluOpType
+ACT = mybir.ActivationFunctionType
+
+P = 128
+H = 4
+DV = 128
+LQ = 1024
+D = 2048
+NT = LQ // P
+N_CHUNK = 512
+NC = D // N_CHUNK
+LN_EPS = 1e-5
+
+FLOPS = 2 * LQ * H * DV * D
+
+
+def tile_multiheadattention_pb_kernel(tc, attn_out, residual, proj_w, proj_b, ln_g, ln_b, out):
+    nc = tc.nc
+    with ExitStack() as ctx:
+        keep = ctx.enter_context(tc.tile_pool(name="keep", bufs=1))
+        work = ctx.enter_context(tc.tile_pool(name="work", bufs=3))
+        small = ctx.enter_context(tc.tile_pool(name="small", bufs=4))
+        psum_x = ctx.enter_context(tc.psum_pool(name="psum_x", bufs=2))
+        psum_z = ctx.enter_context(tc.psum_pool(name="psum_z", bufs=6))
+
+        x_raw = keep.tile([P, H, NT, DV], BF16)
+        nc.sync.dma_start(
+            out=x_raw[:].rearrange("p h t j -> p h (t j)"),
+            in_=attn_out.rearrange("h (p t) j -> p h (t j)", t=NT),
+        )
+        w_raw = keep.tile([P, H, D], BF16)
+        w_view = proj_w.rearrange("(h q) n -> q h n", q=P)
+        for c in range(NC):
+            cols = slice(c * N_CHUNK, (c + 1) * N_CHUNK)
+            nc.sync.dma_start(out=w_raw[:, :, cols], in_=w_view[:, :, cols])
+        bias_bc = keep.tile([P, D], BF16)
+        nc.sync.dma_start(out=bias_bc[:], in_=proj_b.partition_broadcast(P))
+        r_sb = keep.tile([P, NT, D], BF16)
+        r_view = residual.rearrange("(p t) n -> p t n", t=NT)
+        nc.sync.dma_start(out=r_sb[:, 0:2, :], in_=r_view[:, 0:2, :])
+        gain_bc = keep.tile([P, D], BF16)
+        nc.sync.dma_start(out=gain_bc[:], in_=ln_g.partition_broadcast(P))
+        shift_bc = keep.tile([P, D], BF16)
+        nc.sync.dma_start(out=shift_bc[:], in_=ln_b.partition_broadcast(P))
+        for t in range(2, NT, 2):
+            nc.sync.dma_start(out=r_sb[:, t : t + 2, :], in_=r_view[:, t : t + 2, :])
+
+        ident = keep.tile([P, P], BF16)
+        make_identity(nc, ident[:])
+        eps = keep.tile([P, 1], F32)
+        nc.vector.memset(eps[:], LN_EPS)
+
+        x_grouped = keep.tile([P, NT, P, H], BF16, align_bytes=64)
+        x_codes = keep.tile([P, NT * P], U32, align_bytes=64)
+        x_scales = keep.tile([P, NT * P], U8, align_bytes=64)
+        for t in range(NT):
+            toks = slice(t * P, (t + 1) * P)
+            xt = psum_x.tile([P, H, P], BF16)
+            for h in range(H):
+                nc.tensor.transpose(xt[:, h, :], x_raw[:, h, t, :], ident[:])
+            nc.scalar.copy(out=x_grouped[:, t, :, :], in_=xt[:].rearrange("q h p -> q p h"))
+            nc.vector.quantize_mx(
+                out=x_codes[:, toks].bitcast(FP8X4),
+                scales=x_scales[:, toks],
+                in_=x_grouped[:, t, :, :].rearrange("q p h -> q (p h)"),
+            )
+
+        w_grouped = keep.tile([P, D, H], BF16, align_bytes=64)
+        w_codes = keep.tile([P, D], U32, align_bytes=64)
+        w_scales = keep.tile([P, D], U8, align_bytes=64)
+        for c in range(NC):
+            cols = slice(c * N_CHUNK, (c + 1) * N_CHUNK)
+            src = w_raw[:, :, cols].rearrange("q h n -> q n h")
+            if c % 2 == 0:
+                nc.vector.tensor_copy(out=w_grouped[:, cols, :], in_=src)
+            else:
+                nc.scalar.copy(out=w_grouped[:, cols, :], in_=src)
+            nc.vector.quantize_mx(
+                out=w_codes[:, cols].bitcast(FP8X4),
+                scales=w_scales[:, cols],
+                in_=w_grouped[:, cols, :].rearrange("q n h -> q (n h)"),
+            )
+
+        out_view = out.rearrange("(p t) n -> p t n", t=NT)
+        for t in range(NT):
+            toks = slice(t * P, (t + 1) * P)
+            y = work.tile([P, D], F32)
+            for c in range(NC):
+                cols = slice(c * N_CHUNK, (c + 1) * N_CHUNK)
+                z = psum_z.tile([P, N_CHUNK], F32)
+                nc.tensor.matmul_mx(
+                    out=z[:],
+                    lhsT=x_codes[:, toks].bitcast(FP8X4),
+                    lhsT_scale=x_scales[:, toks],
+                    rhs=w_codes[:, cols].bitcast(FP8X4),
+                    rhs_scale=w_scales[:, cols],
+                    start=True,
+                    stop=True,
+                )
+                nc.vector.tensor_tensor(out=y[:, cols], in0=z[:], in1=r_sb[:, t, cols], op=ALU.add)
+            row_sum = small.tile([P, 1], F32)
+            nc.vector.scalar_tensor_tensor(
+                out=y[:], in0=y[:], scalar=0.0, in1=bias_bc[:], op0=ALU.add, op1=ALU.add, accum_out=row_sum[:]
+            )
+            neg_mean = small.tile([P, 1], F32)
+            nc.vector.tensor_scalar_mul(out=neg_mean[:], in0=row_sum[:], scalar1=-1.0 / D)
+            squares = work.tile([P, D], BF16)
+            sq_sum = small.tile([P, 1], F32)
+            nc.scalar.activation(
+                out=squares[:], in_=y[:], func=ACT.Square, bias=neg_mean[:], scale=1.0, accum_out=sq_sum[:]
+            )
+            std = small.tile([P, 1], F32)
+            nc.scalar.activation(out=std[:], in_=sq_sum[:], func=ACT.Sqrt, bias=eps[:], scale=1.0 / D)
+            rstd = small.tile([P, 1], F32)
+            nc.vector.reciprocal(out=rstd[:], in_=std[:])
+            o = work.tile([P, D], F32)
+            nc.vector.scalar_tensor_tensor(
+                out=o[:], in0=y[:], scalar=neg_mean[:], in1=gain_bc[:], op0=ALU.add, op1=ALU.mult
+            )
+            nc.vector.scalar_tensor_tensor(
+                out=o[:], in0=o[:], scalar=rstd[:], in1=shift_bc[:], op0=ALU.mult, op1=ALU.add
+            )
+            nc.sync.dma_start(out=out_view[:, t, :], in_=o[:])

@@ -10,6 +10,7 @@ U8 = mybir.dt.uint8
 FP8X4 = mybir.dt.float8_e4m3fn_x4
 ALU = mybir.AluOpType
 ACT = mybir.ActivationFunctionType
+AX = mybir.AxisListType
 
 P = 128
 H = 4
@@ -17,9 +18,14 @@ DV = 128
 LQ = 1024
 D = 2048
 NT = LQ // P
+NF = D // P
 N_CHUNK = 512
 NC = D // N_CHUNK
+F_PER_CHUNK = N_CHUNK // P
+TG = 2
+NG = NT // TG
 LN_EPS = 1e-5
+G_ROW = 32
 
 FLOPS = 2 * LQ * H * DV * D
 
@@ -28,11 +34,17 @@ def tile_multiheadattention_pb_kernel(tc, attn_out, residual, proj_w, proj_b, ln
     nc = tc.nc
     with ExitStack() as ctx:
         keep = ctx.enter_context(tc.tile_pool(name="keep", bufs=1))
-        work = ctx.enter_context(tc.tile_pool(name="work", bufs=3))
+        work = ctx.enter_context(tc.tile_pool(name="work", bufs=2))
         small = ctx.enter_context(tc.tile_pool(name="small", bufs=4))
-        psum_x = ctx.enter_context(tc.psum_pool(name="psum_x", bufs=2))
-        psum_z = ctx.enter_context(tc.psum_pool(name="psum_z", bufs=6))
+        psum_z = ctx.enter_context(tc.psum_pool(name="psum_z", bufs=2))
+        psum_t = ctx.enter_context(tc.psum_pool(name="psum_t", bufs=2))
+        psum_v = ctx.enter_context(tc.psum_pool(name="psum_v", bufs=1))
+        psum_n = ctx.enter_context(tc.psum_pool(name="psum_n", bufs=3))
 
+        vec_rows = keep.tile([P, P], BF16)
+        nc.vector.memset(vec_rows[:], 0.0)
+        nc.sync.dma_start(out=vec_rows[0:NF, :], in_=proj_b.rearrange("(j q) -> j q", q=P))
+        nc.sync.dma_start(out=vec_rows[G_ROW : G_ROW + NF, :], in_=ln_g.rearrange("(j q) -> j q", q=P))
         x_raw = keep.tile([P, H, NT, DV], BF16)
         nc.sync.dma_start(
             out=x_raw[:].rearrange("p h t j -> p h (t j)"),
@@ -43,31 +55,49 @@ def tile_multiheadattention_pb_kernel(tc, attn_out, residual, proj_w, proj_b, ln
         for c in range(NC):
             cols = slice(c * N_CHUNK, (c + 1) * N_CHUNK)
             nc.sync.dma_start(out=w_raw[:, :, cols], in_=w_view[:, :, cols])
-        bias_bc = keep.tile([P, D], BF16)
-        nc.sync.dma_start(out=bias_bc[:], in_=proj_b.partition_broadcast(P))
         r_sb = keep.tile([P, NT, D], BF16)
         r_view = residual.rearrange("(p t) n -> p t n", t=NT)
-        nc.sync.dma_start(out=r_sb[:, 0:2, :], in_=r_view[:, 0:2, :])
-        gain_bc = keep.tile([P, D], BF16)
-        nc.sync.dma_start(out=gain_bc[:], in_=ln_g.partition_broadcast(P))
         shift_bc = keep.tile([P, D], BF16)
-        nc.sync.dma_start(out=shift_bc[:], in_=ln_b.partition_broadcast(P))
-        for t in range(2, NT, 2):
-            nc.sync.dma_start(out=r_sb[:, t : t + 2, :], in_=r_view[:, t : t + 2, :])
+        for g in range(NG):
+            tiles = slice(g * TG, (g + 1) * TG)
+            nc.sync.dma_start(out=r_sb[:, tiles, :], in_=r_view[:, tiles, :])
+            if g == 1:
+                nc.sync.dma_start(out=shift_bc[:], in_=ln_b.partition_broadcast(P))
 
-        ident = keep.tile([P, P], BF16)
-        make_identity(nc, ident[:])
         eps = keep.tile([P, 1], F32)
         nc.vector.memset(eps[:], LN_EPS)
+        warm = keep.tile([P, 1], F32)
+        nc.scalar.activation(out=warm[:], in_=eps[:], func=ACT.Sqrt)
+        ident_b = keep.tile([P, P], BF16)
+        make_identity(nc, ident_b[:])
+        ident_f = keep.tile([P, P], F32)
+        make_identity(nc, ident_f[:])
+        ones_b = keep.tile([P, P], BF16)
+        nc.vector.memset(ones_b[:], 1.0)
+
+        vec_ps = psum_n.tile([P, P], BF16, tag="pn")
+        nc.tensor.transpose(vec_ps[:], vec_rows[:], ident_b[:])
+        vec_cols_b = keep.tile([P, P], BF16)
+        nc.vector.tensor_copy(out=vec_cols_b[:], in_=vec_ps[:])
+        vec_cols = keep.tile([P, P], F32)
+        nc.vector.tensor_copy(out=vec_cols[:], in_=vec_ps[:])
+        bias_col = vec_cols[:, 0:NF]
+        gain_col = vec_cols[:, G_ROW : G_ROW + NF]
+        gain_bias_col = keep.tile([P, NF], F32)
+        nc.vector.tensor_tensor(out=gain_bias_col[:], in0=gain_col, in1=bias_col, op=ALU.mult)
+        sum_ps = psum_n.tile([P, P], F32, tag="pn")
+        nc.tensor.matmul(out=sum_ps[:], lhsT=ones_b[:], rhs=vec_cols_b[:], start=True, stop=True)
+        bias_sum = keep.tile([P, 1], F32)
+        nc.vector.tensor_reduce(out=bias_sum[:], in_=sum_ps[:, 0:NF], axis=AX.X, op=ALU.add)
 
         x_grouped = keep.tile([P, NT, P, H], BF16, align_bytes=64)
         x_codes = keep.tile([P, NT * P], U32, align_bytes=64)
         x_scales = keep.tile([P, NT * P], U8, align_bytes=64)
         for t in range(NT):
             toks = slice(t * P, (t + 1) * P)
-            xt = psum_x.tile([P, H, P], BF16)
+            xt = psum_n.tile([P, H, P], BF16, tag="pn")
             for h in range(H):
-                nc.tensor.transpose(xt[:, h, :], x_raw[:, h, t, :], ident[:])
+                nc.tensor.transpose(xt[:, h, :], x_raw[:, h, t, :], ident_b[:])
             nc.scalar.copy(out=x_grouped[:, t, :, :], in_=xt[:].rearrange("q h p -> q p h"))
             nc.vector.quantize_mx(
                 out=x_codes[:, toks].bitcast(FP8X4),
@@ -80,11 +110,11 @@ def tile_multiheadattention_pb_kernel(tc, attn_out, residual, proj_w, proj_b, ln
         w_scales = keep.tile([P, D], U8, align_bytes=64)
         for c in range(NC):
             cols = slice(c * N_CHUNK, (c + 1) * N_CHUNK)
-            src = w_raw[:, :, cols].rearrange("q h n -> q n h")
+            w_rows = w_raw[:, :, cols].rearrange("q h n -> q n h")
             if c % 2 == 0:
-                nc.vector.tensor_copy(out=w_grouped[:, cols, :], in_=src)
+                nc.vector.tensor_copy(out=w_grouped[:, cols, :], in_=w_rows)
             else:
-                nc.scalar.copy(out=w_grouped[:, cols, :], in_=src)
+                nc.scalar.copy(out=w_grouped[:, cols, :], in_=w_rows)
             nc.vector.quantize_mx(
                 out=w_codes[:, cols].bitcast(FP8X4),
                 scales=w_scales[:, cols],
@@ -92,42 +122,111 @@ def tile_multiheadattention_pb_kernel(tc, attn_out, residual, proj_w, proj_b, ln
             )
 
         out_view = out.rearrange("(p t) n -> p t n", t=NT)
-        for t in range(NT):
-            toks = slice(t * P, (t + 1) * P)
-            y = work.tile([P, D], F32)
-            for c in range(NC):
-                cols = slice(c * N_CHUNK, (c + 1) * N_CHUNK)
-                z = psum_z.tile([P, N_CHUNK], F32)
-                nc.tensor.matmul_mx(
-                    out=z[:],
-                    lhsT=x_codes[:, toks].bitcast(FP8X4),
-                    lhsT_scale=x_scales[:, toks],
-                    rhs=w_codes[:, cols].bitcast(FP8X4),
-                    rhs_scale=w_scales[:, cols],
-                    start=True,
-                    stop=True,
+
+        def stage_a(g):
+            yc = work.tile([P, TG, D], F32, name="yc")
+            for i in range(TG):
+                t = g * TG + i
+                toks = slice(t * P, (t + 1) * P)
+                chunk_sums = small.tile([P, NC], F32, name="chunk_sums")
+                for c in range(NC):
+                    cols = slice(c * N_CHUNK, (c + 1) * N_CHUNK)
+                    z = psum_z.tile([P, N_CHUNK], F32, name="z")
+                    nc.tensor.matmul_mx(
+                        out=z[:],
+                        lhsT=x_codes[:, toks].bitcast(FP8X4),
+                        lhsT_scale=x_scales[:, toks],
+                        rhs=w_codes[:, cols].bitcast(FP8X4),
+                        rhs_scale=w_scales[:, cols],
+                        start=True,
+                        stop=True,
+                    )
+                    nc.vector.scalar_tensor_tensor(
+                        out=yc[:, i, cols],
+                        in0=z[:],
+                        scalar=0.0,
+                        in1=r_sb[:, t, cols],
+                        op0=ALU.add,
+                        op1=ALU.add,
+                        accum_out=chunk_sums[:, c : c + 1],
+                    )
+                row_sum = small.tile([P, 1], F32, name="row_sum")
+                nc.vector.tensor_reduce(out=row_sum[:], in_=chunk_sums[:], axis=AX.X, op=ALU.add)
+                neg_mean = small.tile([P, 1], F32, name="neg_mean")
+                nc.vector.tensor_scalar(
+                    out=neg_mean[:], in0=row_sum[:], scalar1=bias_sum[:], scalar2=-1.0 / D, op0=ALU.add, op1=ALU.mult
                 )
-                nc.vector.tensor_tensor(out=y[:, cols], in0=z[:], in1=r_sb[:, t, cols], op=ALU.add)
-            row_sum = small.tile([P, 1], F32)
-            nc.vector.scalar_tensor_tensor(
-                out=y[:], in0=y[:], scalar=0.0, in1=bias_bc[:], op0=ALU.add, op1=ALU.add, accum_out=row_sum[:]
-            )
-            neg_mean = small.tile([P, 1], F32)
-            nc.vector.tensor_scalar_mul(out=neg_mean[:], in0=row_sum[:], scalar1=-1.0 / D)
-            squares = work.tile([P, D], BF16)
-            sq_sum = small.tile([P, 1], F32)
-            nc.scalar.activation(
-                out=squares[:], in_=y[:], func=ACT.Square, bias=neg_mean[:], scale=1.0, accum_out=sq_sum[:]
-            )
-            std = small.tile([P, 1], F32)
+                nc.gpsimd.tensor_scalar(
+                    out=yc[:, i, :], in0=yc[:, i, :], scalar1=1.0, scalar2=neg_mean[:], op0=ALU.mult, op1=ALU.add
+                )
+            return yc
+
+        def stage_b(yc):
+            squares = work.tile([P, NF, TG * P], F32, name="squares")
+            scaled = work.tile([P, NF, TG * P], F32, name="scaled")
+            for j0 in range(0, NF, 2):
+                yct = psum_t.tile([P, 2, TG * P], F32, name="yct")
+                for jj in range(2):
+                    feats = slice((j0 + jj) * P, (j0 + jj + 1) * P)
+                    for i in range(TG):
+                        nc.tensor.transpose(yct[:, jj, i * P : (i + 1) * P], yc[:, i, feats], ident_f[:])
+                for jj in range(2):
+                    j = j0 + jj
+                    nc.scalar.activation(
+                        out=squares[:, j, :], in_=yct[:, jj, :], func=ACT.Square, bias=bias_col[:, j : j + 1], scale=1.0
+                    )
+                    nc.scalar.activation(
+                        out=scaled[:, j, :],
+                        in_=yct[:, jj, :],
+                        func=ACT.Identity,
+                        bias=gain_bias_col[:, j : j + 1],
+                        scale=gain_col[:, j : j + 1],
+                    )
+            return squares, scaled
+
+        def stage_c(g, squares, scaled):
+            sq_acc = psum_v.tile([P, TG, P], F32, name="sq_acc")
+            for i in range(TG):
+                toks = slice(i * P, (i + 1) * P)
+                for j in range(NF):
+                    nc.tensor.matmul(
+                        out=sq_acc[:, i, :],
+                        lhsT=squares[:, j, toks],
+                        rhs=ident_f[:],
+                        is_transpose=True,
+                        start=(j == 0),
+                        stop=(j == NF - 1),
+                    )
+            sq_sum = small.tile([P, TG], F32, name="sq_sum")
+            nc.vector.tensor_reduce(out=sq_sum[:], in_=sq_acc[:], axis=AX.X, op=ALU.add)
+            std = small.tile([P, TG], F32, name="std")
             nc.scalar.activation(out=std[:], in_=sq_sum[:], func=ACT.Sqrt, bias=eps[:], scale=1.0 / D)
-            rstd = small.tile([P, 1], F32)
+            rstd = small.tile([P, TG], F32, name="rstd")
             nc.vector.reciprocal(out=rstd[:], in_=std[:])
-            o = work.tile([P, D], F32)
-            nc.vector.scalar_tensor_tensor(
-                out=o[:], in0=y[:], scalar=neg_mean[:], in1=gain_bc[:], op0=ALU.add, op1=ALU.mult
-            )
-            nc.vector.scalar_tensor_tensor(
-                out=o[:], in0=o[:], scalar=rstd[:], in1=shift_bc[:], op0=ALU.mult, op1=ALU.add
-            )
-            nc.sync.dma_start(out=out_view[:, t, :], in_=o[:])
+            o = work.tile([P, TG, D], F32, name="o")
+            for i in range(TG):
+                toks = slice(i * P, (i + 1) * P)
+                for c in range(NC):
+                    cols = slice(c * N_CHUNK, (c + 1) * N_CHUNK)
+                    back = psum_n.tile([P, N_CHUNK], F32, name="back", tag="pn")
+                    for jj in range(F_PER_CHUNK):
+                        nc.tensor.transpose(
+                            back[:, jj * P : (jj + 1) * P], scaled[:, c * F_PER_CHUNK + jj, toks], ident_f[:]
+                        )
+                    nc.vector.scalar_tensor_tensor(
+                        out=o[:, i, cols],
+                        in0=back[:],
+                        scalar=rstd[:, i : i + 1],
+                        in1=shift_bc[:, cols],
+                        op0=ALU.mult,
+                        op1=ALU.add,
+                    )
+            nc.sync.dma_start(out=out_view[:, g * TG : (g + 1) * TG, :], in_=o[:])
+
+        yc_next = stage_a(0)
+        for g in range(NG):
+            yc_now = yc_next
+            if g + 1 < NG:
+                yc_next = stage_a(g + 1)
+            squares, scaled = stage_b(yc_now)
+            stage_c(g, squares, scaled)

@@ -19,13 +19,12 @@ LQ = 1024
 D = 2048
 NT = LQ // P
 NF = D // P
-N_CHUNK = 512
-NC = D // N_CHUNK
-F_PER_CHUNK = N_CHUNK // P
-TG = 2
-NG = NT // TG
+BANK = 512
+NC = D // BANK
+F_PER_CHUNK = BANK // P
+T_PER_PASS = BANK // P
+NQ = NT // T_PER_PASS
 LN_EPS = 1e-5
-G_ROW = 32
 
 FLOPS = 2 * LQ * H * DV * D
 
@@ -34,17 +33,15 @@ def tile_multiheadattention_pb_kernel(tc, attn_out, residual, proj_w, proj_b, ln
     nc = tc.nc
     with ExitStack() as ctx:
         keep = ctx.enter_context(tc.tile_pool(name="keep", bufs=1))
-        work = ctx.enter_context(tc.tile_pool(name="work", bufs=2))
+        rows = ctx.enter_context(tc.tile_pool(name="rows", bufs=2))
+        work = ctx.enter_context(tc.tile_pool(name="work", bufs=3))
         small = ctx.enter_context(tc.tile_pool(name="small", bufs=4))
-        psum_z = ctx.enter_context(tc.psum_pool(name="psum_z", bufs=2))
-        psum_t = ctx.enter_context(tc.psum_pool(name="psum_t", bufs=2))
-        psum_v = ctx.enter_context(tc.psum_pool(name="psum_v", bufs=1))
-        psum_n = ctx.enter_context(tc.psum_pool(name="psum_n", bufs=3))
+        psum_f = ctx.enter_context(tc.psum_pool(name="psum_f", bufs=3))
+        psum_t = ctx.enter_context(tc.psum_pool(name="psum_t", bufs=5))
 
-        vec_rows = keep.tile([P, P], BF16)
-        nc.vector.memset(vec_rows[:], 0.0)
-        nc.sync.dma_start(out=vec_rows[0:NF, :], in_=proj_b.rearrange("(j q) -> j q", q=P))
-        nc.sync.dma_start(out=vec_rows[G_ROW : G_ROW + NF, :], in_=ln_g.rearrange("(j q) -> j q", q=P))
+        bias_rows = keep.tile([P, P], BF16)
+        nc.vector.memset(bias_rows[:], 0.0)
+        nc.sync.dma_start(out=bias_rows[0:NF, :], in_=proj_b.rearrange("(j q) -> j q", q=P))
         x_raw = keep.tile([P, H, NT, DV], BF16)
         nc.sync.dma_start(
             out=x_raw[:].rearrange("p h t j -> p h (t j)"),
@@ -52,17 +49,19 @@ def tile_multiheadattention_pb_kernel(tc, attn_out, residual, proj_w, proj_b, ln
         )
         w_raw = keep.tile([P, H, D], BF16)
         w_view = proj_w.rearrange("(h q) n -> q h n", q=P)
-        for c in range(NC):
-            cols = slice(c * N_CHUNK, (c + 1) * N_CHUNK)
-            nc.sync.dma_start(out=w_raw[:, :, cols], in_=w_view[:, :, cols])
         r_sb = keep.tile([P, NT, D], BF16)
         r_view = residual.rearrange("(p t) n -> p t n", t=NT)
+        first_half = slice(0, T_PER_PASS)
+        second_half = slice(T_PER_PASS, NT)
+        for c in range(NC):
+            cols = slice(c * BANK, (c + 1) * BANK)
+            nc.sync.dma_start(out=w_raw[:, :, cols], in_=w_view[:, :, cols])
+            nc.sync.dma_start(out=r_sb[:, first_half, cols], in_=r_view[:, first_half, cols])
+        nc.sync.dma_start(out=r_sb[:, second_half, :], in_=r_view[:, second_half, :])
+        gain_bc = keep.tile([P, D], BF16)
+        nc.sync.dma_start(out=gain_bc[:], in_=ln_g.partition_broadcast(P))
         shift_bc = keep.tile([P, D], BF16)
-        for g in range(NG):
-            tiles = slice(g * TG, (g + 1) * TG)
-            nc.sync.dma_start(out=r_sb[:, tiles, :], in_=r_view[:, tiles, :])
-            if g == 1:
-                nc.sync.dma_start(out=shift_bc[:], in_=ln_b.partition_broadcast(P))
+        nc.sync.dma_start(out=shift_bc[:], in_=ln_b.partition_broadcast(P))
 
         eps = keep.tile([P, 1], F32)
         nc.vector.memset(eps[:], LN_EPS)
@@ -72,44 +71,33 @@ def tile_multiheadattention_pb_kernel(tc, attn_out, residual, proj_w, proj_b, ln
         make_identity(nc, ident_b[:])
         ident_f = keep.tile([P, P], F32)
         make_identity(nc, ident_f[:])
-        ones_b = keep.tile([P, P], BF16)
-        nc.vector.memset(ones_b[:], 1.0)
-
-        vec_ps = psum_n.tile([P, P], BF16, tag="pn")
-        nc.tensor.transpose(vec_ps[:], vec_rows[:], ident_b[:])
-        vec_cols_b = keep.tile([P, P], BF16)
-        nc.vector.tensor_copy(out=vec_cols_b[:], in_=vec_ps[:])
-        vec_cols = keep.tile([P, P], F32)
-        nc.vector.tensor_copy(out=vec_cols[:], in_=vec_ps[:])
-        bias_col = vec_cols[:, 0:NF]
-        gain_col = vec_cols[:, G_ROW : G_ROW + NF]
-        gain_bias_col = keep.tile([P, NF], F32)
-        nc.vector.tensor_tensor(out=gain_bias_col[:], in0=gain_col, in1=bias_col, op=ALU.mult)
-        sum_ps = psum_n.tile([P, P], F32, tag="pn")
-        nc.tensor.matmul(out=sum_ps[:], lhsT=ones_b[:], rhs=vec_cols_b[:], start=True, stop=True)
-        bias_sum = keep.tile([P, 1], F32)
-        nc.vector.tensor_reduce(out=bias_sum[:], in_=sum_ps[:, 0:NF], axis=AX.X, op=ALU.add)
 
         x_grouped = keep.tile([P, NT, P, H], BF16, align_bytes=64)
         x_codes = keep.tile([P, NT * P], U32, align_bytes=64)
         x_scales = keep.tile([P, NT * P], U8, align_bytes=64)
-        for t in range(NT):
-            toks = slice(t * P, (t + 1) * P)
-            xt = psum_n.tile([P, H, P], BF16, tag="pn")
-            for h in range(H):
-                nc.tensor.transpose(xt[:, h, :], x_raw[:, h, t, :], ident_b[:])
-            nc.scalar.copy(out=x_grouped[:, t, :, :], in_=xt[:].rearrange("q h p -> q p h"))
+        for g in range(NQ):
+            for t in range(g * T_PER_PASS, (g + 1) * T_PER_PASS):
+                xt = psum_t.tile([P, H, P], BF16, tag="tok")
+                for h in range(H):
+                    nc.tensor.transpose(xt[:, h, :], x_raw[:, h, t, :], ident_b[:])
+                nc.scalar.copy(out=x_grouped[:, t, :, :], in_=xt[:].rearrange("q h p -> q p h"))
+            toks = slice(g * BANK, (g + 1) * BANK)
             nc.vector.quantize_mx(
                 out=x_codes[:, toks].bitcast(FP8X4),
                 scales=x_scales[:, toks],
-                in_=x_grouped[:, t, :, :].rearrange("q p h -> q (p h)"),
+                in_=x_grouped[:, g * T_PER_PASS : (g + 1) * T_PER_PASS, :, :].rearrange("q t p h -> q (t p h)"),
             )
+
+        bias_ps = psum_t.tile([P, P], BF16, tag="tok")
+        nc.tensor.transpose(bias_ps[:], bias_rows[:], ident_b[:])
+        bias_col = keep.tile([P, NF], F32)
+        nc.vector.tensor_copy(out=bias_col[:], in_=bias_ps[:, 0:NF])
 
         w_grouped = keep.tile([P, D, H], BF16, align_bytes=64)
         w_codes = keep.tile([P, D], U32, align_bytes=64)
         w_scales = keep.tile([P, D], U8, align_bytes=64)
         for c in range(NC):
-            cols = slice(c * N_CHUNK, (c + 1) * N_CHUNK)
+            cols = slice(c * BANK, (c + 1) * BANK)
             w_rows = w_raw[:, :, cols].rearrange("q h n -> q n h")
             if c % 2 == 0:
                 nc.vector.tensor_copy(out=w_grouped[:, cols, :], in_=w_rows)
@@ -123,110 +111,74 @@ def tile_multiheadattention_pb_kernel(tc, attn_out, residual, proj_w, proj_b, ln
 
         out_view = out.rearrange("(p t) n -> p t n", t=NT)
 
-        def stage_a(g):
-            yc = work.tile([P, TG, D], F32, name="yc")
-            for i in range(TG):
-                t = g * TG + i
-                toks = slice(t * P, (t + 1) * P)
-                chunk_sums = small.tile([P, NC], F32, name="chunk_sums")
-                for c in range(NC):
-                    cols = slice(c * N_CHUNK, (c + 1) * N_CHUNK)
-                    z = psum_z.tile([P, N_CHUNK], F32, name="z")
+        def project(g):
+            toks = slice(g * BANK, (g + 1) * BANK)
+            y = rows.tile([P, T_PER_PASS, D], F32, name="y")
+            chunk_sums = small.tile([P, T_PER_PASS, NC], F32, name="chunk_sums")
+            for c in range(NC):
+                cols = slice(c * BANK, (c + 1) * BANK)
+                zb = work.tile([P, F_PER_CHUNK, BANK], F32, name="zb")
+                for jj in range(F_PER_CHUNK):
+                    j = c * F_PER_CHUNK + jj
+                    feats = slice(j * P, (j + 1) * P)
+                    z = psum_f.tile([P, BANK], F32, name="z")
                     nc.tensor.matmul_mx(
                         out=z[:],
-                        lhsT=x_codes[:, toks].bitcast(FP8X4),
-                        lhsT_scale=x_scales[:, toks],
-                        rhs=w_codes[:, cols].bitcast(FP8X4),
-                        rhs_scale=w_scales[:, cols],
+                        lhsT=w_codes[:, feats].bitcast(FP8X4),
+                        lhsT_scale=w_scales[:, feats],
+                        rhs=x_codes[:, toks].bitcast(FP8X4),
+                        rhs_scale=x_scales[:, toks],
                         start=True,
                         stop=True,
                     )
+                    nc.scalar.activation(
+                        out=zb[:, jj, :], in_=z[:], func=ACT.Identity, bias=bias_col[:, j : j + 1], scale=1.0
+                    )
+                for i in range(T_PER_PASS):
+                    zbt = psum_t.tile([P, BANK], F32, name="zbt", tag="tok")
+                    for jj in range(F_PER_CHUNK):
+                        nc.tensor.transpose(zbt[:, jj * P : (jj + 1) * P], zb[:, jj, i * P : (i + 1) * P], ident_f[:])
                     nc.vector.scalar_tensor_tensor(
-                        out=yc[:, i, cols],
-                        in0=z[:],
+                        out=y[:, i, cols],
+                        in0=zbt[:],
                         scalar=0.0,
-                        in1=r_sb[:, t, cols],
+                        in1=r_sb[:, g * T_PER_PASS + i, cols],
                         op0=ALU.add,
                         op1=ALU.add,
-                        accum_out=chunk_sums[:, c : c + 1],
+                        accum_out=chunk_sums[:, i, c : c + 1],
                     )
-                row_sum = small.tile([P, 1], F32, name="row_sum")
-                nc.vector.tensor_reduce(out=row_sum[:], in_=chunk_sums[:], axis=AX.X, op=ALU.add)
-                neg_mean = small.tile([P, 1], F32, name="neg_mean")
-                nc.vector.tensor_scalar(
-                    out=neg_mean[:], in0=row_sum[:], scalar1=bias_sum[:], scalar2=-1.0 / D, op0=ALU.add, op1=ALU.mult
+            return y, chunk_sums
+
+        def normalise(g, y, chunk_sums):
+            row_sum = small.tile([P, T_PER_PASS], F32, name="row_sum")
+            nc.vector.tensor_reduce(out=row_sum[:], in_=chunk_sums[:], axis=AX.X, op=ALU.add)
+            neg_mean = small.tile([P, T_PER_PASS], F32, name="neg_mean")
+            nc.vector.tensor_scalar_mul(out=neg_mean[:], in0=row_sum[:], scalar1=-1.0 / D)
+            for i in range(T_PER_PASS):
+                squares = work.tile([P, D], BF16, name="squares")
+                sq_sum = small.tile([P, 1], F32, name="sq_sum")
+                nc.scalar.activation(
+                    out=squares[:],
+                    in_=y[:, i, :],
+                    func=ACT.Square,
+                    bias=neg_mean[:, i : i + 1],
+                    scale=1.0,
+                    accum_out=sq_sum[:],
                 )
-                nc.gpsimd.tensor_scalar(
-                    out=yc[:, i, :], in0=yc[:, i, :], scalar1=1.0, scalar2=neg_mean[:], op0=ALU.mult, op1=ALU.add
+                std = small.tile([P, 1], F32, name="std")
+                nc.scalar.activation(out=std[:], in_=sq_sum[:], func=ACT.Sqrt, bias=eps[:], scale=1.0 / D)
+                rstd = small.tile([P, 1], F32, name="rstd")
+                nc.vector.reciprocal(out=rstd[:], in_=std[:])
+                o = work.tile([P, D], F32, name="o")
+                nc.vector.scalar_tensor_tensor(
+                    out=o[:], in0=y[:, i, :], scalar=neg_mean[:, i : i + 1], in1=gain_bc[:], op0=ALU.add, op1=ALU.mult
                 )
-            return yc
+                nc.vector.scalar_tensor_tensor(
+                    out=o[:], in0=o[:], scalar=rstd[:], in1=shift_bc[:], op0=ALU.mult, op1=ALU.add
+                )
+                nc.sync.dma_start(out=out_view[:, g * T_PER_PASS + i, :], in_=o[:])
 
-        def stage_b(yc):
-            squares = work.tile([P, NF, TG * P], F32, name="squares")
-            scaled = work.tile([P, NF, TG * P], F32, name="scaled")
-            for j0 in range(0, NF, 2):
-                yct = psum_t.tile([P, 2, TG * P], F32, name="yct")
-                for jj in range(2):
-                    feats = slice((j0 + jj) * P, (j0 + jj + 1) * P)
-                    for i in range(TG):
-                        nc.tensor.transpose(yct[:, jj, i * P : (i + 1) * P], yc[:, i, feats], ident_f[:])
-                for jj in range(2):
-                    j = j0 + jj
-                    nc.scalar.activation(
-                        out=squares[:, j, :], in_=yct[:, jj, :], func=ACT.Square, bias=bias_col[:, j : j + 1], scale=1.0
-                    )
-                    nc.scalar.activation(
-                        out=scaled[:, j, :],
-                        in_=yct[:, jj, :],
-                        func=ACT.Identity,
-                        bias=gain_bias_col[:, j : j + 1],
-                        scale=gain_col[:, j : j + 1],
-                    )
-            return squares, scaled
-
-        def stage_c(g, squares, scaled):
-            sq_acc = psum_v.tile([P, TG, P], F32, name="sq_acc")
-            for i in range(TG):
-                toks = slice(i * P, (i + 1) * P)
-                for j in range(NF):
-                    nc.tensor.matmul(
-                        out=sq_acc[:, i, :],
-                        lhsT=squares[:, j, toks],
-                        rhs=ident_f[:],
-                        is_transpose=True,
-                        start=(j == 0),
-                        stop=(j == NF - 1),
-                    )
-            sq_sum = small.tile([P, TG], F32, name="sq_sum")
-            nc.vector.tensor_reduce(out=sq_sum[:], in_=sq_acc[:], axis=AX.X, op=ALU.add)
-            std = small.tile([P, TG], F32, name="std")
-            nc.scalar.activation(out=std[:], in_=sq_sum[:], func=ACT.Sqrt, bias=eps[:], scale=1.0 / D)
-            rstd = small.tile([P, TG], F32, name="rstd")
-            nc.vector.reciprocal(out=rstd[:], in_=std[:])
-            o = work.tile([P, TG, D], F32, name="o")
-            for i in range(TG):
-                toks = slice(i * P, (i + 1) * P)
-                for c in range(NC):
-                    cols = slice(c * N_CHUNK, (c + 1) * N_CHUNK)
-                    back = psum_n.tile([P, N_CHUNK], F32, name="back", tag="pn")
-                    for jj in range(F_PER_CHUNK):
-                        nc.tensor.transpose(
-                            back[:, jj * P : (jj + 1) * P], scaled[:, c * F_PER_CHUNK + jj, toks], ident_f[:]
-                        )
-                    nc.vector.scalar_tensor_tensor(
-                        out=o[:, i, cols],
-                        in0=back[:],
-                        scalar=rstd[:, i : i + 1],
-                        in1=shift_bc[:, cols],
-                        op0=ALU.mult,
-                        op1=ALU.add,
-                    )
-            nc.sync.dma_start(out=out_view[:, g * TG : (g + 1) * TG, :], in_=o[:])
-
-        yc_next = stage_a(0)
-        for g in range(NG):
-            yc_now = yc_next
-            if g + 1 < NG:
-                yc_next = stage_a(g + 1)
-            squares, scaled = stage_b(yc_now)
-            stage_c(g, squares, scaled)
+        projected = [project(g) for g in range(NQ)]
+        for g in range(NQ):
+            y, chunk_sums = projected[g]
+            normalise(g, y, chunk_sums)

@@ -19,12 +19,13 @@ LQ = 1024
 D = 2048
 NT = LQ // P
 NF = D // P
-BANK = 512
-NC = D // BANK
-F_PER_CHUNK = BANK // P
-T_PER_PASS = BANK // P
-NQ = NT // T_PER_PASS
+N_CHUNK = 512
+NC = D // N_CHUNK
+F_PER_CHUNK = N_CHUNK // P
+TG = 2
+NG = NT // TG
 LN_EPS = 1e-5
+G_ROW = 32
 
 FLOPS = 2 * LQ * H * DV * D
 
@@ -33,15 +34,17 @@ def tile_multiheadattention_pb_kernel(tc, attn_out, residual, proj_w, proj_b, ln
     nc = tc.nc
     with ExitStack() as ctx:
         keep = ctx.enter_context(tc.tile_pool(name="keep", bufs=1))
-        rows = ctx.enter_context(tc.tile_pool(name="rows", bufs=2))
-        work = ctx.enter_context(tc.tile_pool(name="work", bufs=3))
+        work = ctx.enter_context(tc.tile_pool(name="work", bufs=2))
         small = ctx.enter_context(tc.tile_pool(name="small", bufs=4))
-        psum_f = ctx.enter_context(tc.psum_pool(name="psum_f", bufs=3))
-        psum_t = ctx.enter_context(tc.psum_pool(name="psum_t", bufs=5))
+        psum_z = ctx.enter_context(tc.psum_pool(name="psum_z", bufs=2))
+        psum_t = ctx.enter_context(tc.psum_pool(name="psum_t", bufs=2))
+        psum_v = ctx.enter_context(tc.psum_pool(name="psum_v", bufs=1))
+        psum_n = ctx.enter_context(tc.psum_pool(name="psum_n", bufs=3))
 
-        bias_rows = keep.tile([P, P], BF16)
-        nc.vector.memset(bias_rows[:], 0.0)
-        nc.sync.dma_start(out=bias_rows[0:NF, :], in_=proj_b.rearrange("(j q) -> j q", q=P))
+        vec_rows = keep.tile([P, P], BF16)
+        nc.vector.memset(vec_rows[:], 0.0)
+        nc.sync.dma_start(out=vec_rows[0:NF, :], in_=proj_b.rearrange("(j q) -> j q", q=P))
+        nc.sync.dma_start(out=vec_rows[G_ROW : G_ROW + NF, :], in_=ln_g.rearrange("(j q) -> j q", q=P))
         x_raw = keep.tile([P, H, NT, DV], BF16)
         nc.sync.dma_start(
             out=x_raw[:].rearrange("p h t j -> p h (t j)"),
@@ -49,19 +52,17 @@ def tile_multiheadattention_pb_kernel(tc, attn_out, residual, proj_w, proj_b, ln
         )
         w_raw = keep.tile([P, H, D], BF16)
         w_view = proj_w.rearrange("(h q) n -> q h n", q=P)
+        for c in range(NC):
+            cols = slice(c * N_CHUNK, (c + 1) * N_CHUNK)
+            nc.sync.dma_start(out=w_raw[:, :, cols], in_=w_view[:, :, cols])
         r_sb = keep.tile([P, NT, D], BF16)
         r_view = residual.rearrange("(p t) n -> p t n", t=NT)
-        first_half = slice(0, T_PER_PASS)
-        second_half = slice(T_PER_PASS, NT)
-        for c in range(NC):
-            cols = slice(c * BANK, (c + 1) * BANK)
-            nc.sync.dma_start(out=w_raw[:, :, cols], in_=w_view[:, :, cols])
-            nc.sync.dma_start(out=r_sb[:, first_half, cols], in_=r_view[:, first_half, cols])
-        nc.sync.dma_start(out=r_sb[:, second_half, :], in_=r_view[:, second_half, :])
-        gain_bc = keep.tile([P, D], BF16)
-        nc.sync.dma_start(out=gain_bc[:], in_=ln_g.partition_broadcast(P))
         shift_bc = keep.tile([P, D], BF16)
-        nc.sync.dma_start(out=shift_bc[:], in_=ln_b.partition_broadcast(P))
+        for g in range(NG):
+            tiles = slice(g * TG, (g + 1) * TG)
+            nc.sync.dma_start(out=r_sb[:, tiles, :], in_=r_view[:, tiles, :])
+            if g == 1:
+                nc.sync.dma_start(out=shift_bc[:], in_=ln_b.partition_broadcast(P))
 
         eps = keep.tile([P, 1], F32)
         nc.vector.memset(eps[:], LN_EPS)
@@ -71,33 +72,44 @@ def tile_multiheadattention_pb_kernel(tc, attn_out, residual, proj_w, proj_b, ln
         make_identity(nc, ident_b[:])
         ident_f = keep.tile([P, P], F32)
         make_identity(nc, ident_f[:])
+        ones_b = keep.tile([P, P], BF16)
+        nc.vector.memset(ones_b[:], 1.0)
+
+        vec_ps = psum_n.tile([P, P], BF16, tag="pn")
+        nc.tensor.transpose(vec_ps[:], vec_rows[:], ident_b[:])
+        vec_cols_b = keep.tile([P, P], BF16)
+        nc.vector.tensor_copy(out=vec_cols_b[:], in_=vec_ps[:])
+        vec_cols = keep.tile([P, P], F32)
+        nc.vector.tensor_copy(out=vec_cols[:], in_=vec_ps[:])
+        bias_col = vec_cols[:, 0:NF]
+        gain_col = vec_cols[:, G_ROW : G_ROW + NF]
+        gain_bias_col = keep.tile([P, NF], F32)
+        nc.vector.tensor_tensor(out=gain_bias_col[:], in0=gain_col, in1=bias_col, op=ALU.mult)
+        sum_ps = psum_n.tile([P, P], F32, tag="pn")
+        nc.tensor.matmul(out=sum_ps[:], lhsT=ones_b[:], rhs=vec_cols_b[:], start=True, stop=True)
+        bias_sum = keep.tile([P, 1], F32)
+        nc.vector.tensor_reduce(out=bias_sum[:], in_=sum_ps[:, 0:NF], axis=AX.X, op=ALU.add)
 
         x_grouped = keep.tile([P, NT, P, H], BF16, align_bytes=64)
         x_codes = keep.tile([P, NT * P], U32, align_bytes=64)
         x_scales = keep.tile([P, NT * P], U8, align_bytes=64)
-        for g in range(NQ):
-            for t in range(g * T_PER_PASS, (g + 1) * T_PER_PASS):
-                xt = psum_t.tile([P, H, P], BF16, tag="tok")
-                for h in range(H):
-                    nc.tensor.transpose(xt[:, h, :], x_raw[:, h, t, :], ident_b[:])
-                nc.scalar.copy(out=x_grouped[:, t, :, :], in_=xt[:].rearrange("q h p -> q p h"))
-            toks = slice(g * BANK, (g + 1) * BANK)
+        for t in range(NT):
+            toks = slice(t * P, (t + 1) * P)
+            xt = psum_n.tile([P, H, P], BF16, tag="pn")
+            for h in range(H):
+                nc.tensor.transpose(xt[:, h, :], x_raw[:, h, t, :], ident_b[:])
+            nc.scalar.copy(out=x_grouped[:, t, :, :], in_=xt[:].rearrange("q h p -> q p h"))
             nc.vector.quantize_mx(
                 out=x_codes[:, toks].bitcast(FP8X4),
                 scales=x_scales[:, toks],
-                in_=x_grouped[:, g * T_PER_PASS : (g + 1) * T_PER_PASS, :, :].rearrange("q t p h -> q (t p h)"),
+                in_=x_grouped[:, t, :, :].rearrange("q p h -> q (p h)"),
             )
-
-        bias_ps = psum_t.tile([P, P], BF16, tag="tok")
-        nc.tensor.transpose(bias_ps[:], bias_rows[:], ident_b[:])
-        bias_col = keep.tile([P, NF], F32)
-        nc.vector.tensor_copy(out=bias_col[:], in_=bias_ps[:, 0:NF])
 
         w_grouped = keep.tile([P, D, H], BF16, align_bytes=64)
         w_codes = keep.tile([P, D], U32, align_bytes=64)
         w_scales = keep.tile([P, D], U8, align_bytes=64)
         for c in range(NC):
-            cols = slice(c * BANK, (c + 1) * BANK)
+            cols = slice(c * N_CHUNK, (c + 1) * N_CHUNK)
             w_rows = w_raw[:, :, cols].rearrange("q h n -> q n h")
             if c % 2 == 0:
                 nc.vector.tensor_copy(out=w_grouped[:, cols, :], in_=w_rows)
@@ -111,74 +123,142 @@ def tile_multiheadattention_pb_kernel(tc, attn_out, residual, proj_w, proj_b, ln
 
         out_view = out.rearrange("(p t) n -> p t n", t=NT)
 
-        def project(g):
-            toks = slice(g * BANK, (g + 1) * BANK)
-            y = rows.tile([P, T_PER_PASS, D], F32, name="y")
-            chunk_sums = small.tile([P, T_PER_PASS, NC], F32, name="chunk_sums")
-            for c in range(NC):
-                cols = slice(c * BANK, (c + 1) * BANK)
-                zb = work.tile([P, F_PER_CHUNK, BANK], F32, name="zb")
-                for jj in range(F_PER_CHUNK):
-                    j = c * F_PER_CHUNK + jj
-                    feats = slice(j * P, (j + 1) * P)
-                    z = psum_f.tile([P, BANK], F32, name="z")
-                    nc.tensor.matmul_mx(
-                        out=z[:],
-                        lhsT=w_codes[:, feats].bitcast(FP8X4),
-                        lhsT_scale=w_scales[:, feats],
-                        rhs=x_codes[:, toks].bitcast(FP8X4),
-                        rhs_scale=x_scales[:, toks],
-                        start=True,
-                        stop=True,
-                    )
-                    nc.scalar.activation(
-                        out=zb[:, jj, :], in_=z[:], func=ACT.Identity, bias=bias_col[:, j : j + 1], scale=1.0
-                    )
-                for i in range(T_PER_PASS):
-                    zbt = psum_t.tile([P, BANK], F32, name="zbt", tag="tok")
-                    for jj in range(F_PER_CHUNK):
-                        nc.tensor.transpose(zbt[:, jj * P : (jj + 1) * P], zb[:, jj, i * P : (i + 1) * P], ident_f[:])
-                    nc.vector.scalar_tensor_tensor(
-                        out=y[:, i, cols],
-                        in0=zbt[:],
-                        scalar=0.0,
-                        in1=r_sb[:, g * T_PER_PASS + i, cols],
-                        op0=ALU.add,
-                        op1=ALU.add,
-                        accum_out=chunk_sums[:, i, c : c + 1],
-                    )
-            return y, chunk_sums
+        yc_of = {}
+        sums_of = {}
+        squares_of = {}
+        scaled_of = {}
+        acc_of = {}
+        rstd_of = {}
+        o_of = {}
 
-        def normalise(g, y, chunk_sums):
-            row_sum = small.tile([P, T_PER_PASS], F32, name="row_sum")
-            nc.vector.tensor_reduce(out=row_sum[:], in_=chunk_sums[:], axis=AX.X, op=ALU.add)
-            neg_mean = small.tile([P, T_PER_PASS], F32, name="neg_mean")
-            nc.vector.tensor_scalar_mul(out=neg_mean[:], in0=row_sum[:], scalar1=-1.0 / D)
-            for i in range(T_PER_PASS):
-                squares = work.tile([P, D], BF16, name="squares")
-                sq_sum = small.tile([P, 1], F32, name="sq_sum")
+        def project(g, i, c):
+            if i == 0 and c == 0:
+                yc_of[g] = work.tile([P, TG, D], F32, name="yc")
+            if c == 0:
+                sums_of[g, i] = small.tile([P, NC], F32, name="chunk_sums")
+            t = g * TG + i
+            toks = slice(t * P, (t + 1) * P)
+            cols = slice(c * N_CHUNK, (c + 1) * N_CHUNK)
+            z = psum_z.tile([P, N_CHUNK], F32, name="z")
+            nc.tensor.matmul_mx(
+                out=z[:],
+                lhsT=x_codes[:, toks].bitcast(FP8X4),
+                lhsT_scale=x_scales[:, toks],
+                rhs=w_codes[:, cols].bitcast(FP8X4),
+                rhs_scale=w_scales[:, cols],
+                start=True,
+                stop=True,
+            )
+            nc.vector.scalar_tensor_tensor(
+                out=yc_of[g][:, i, cols],
+                in0=z[:],
+                scalar=0.0,
+                in1=r_sb[:, t, cols],
+                op0=ALU.add,
+                op1=ALU.add,
+                accum_out=sums_of[g, i][:, c : c + 1],
+            )
+
+        def centre(g, i):
+            row_sum = small.tile([P, 1], F32, name="row_sum")
+            nc.vector.tensor_reduce(out=row_sum[:], in_=sums_of[g, i][:], axis=AX.X, op=ALU.add)
+            neg_mean = small.tile([P, 1], F32, name="neg_mean")
+            nc.vector.tensor_scalar(
+                out=neg_mean[:], in0=row_sum[:], scalar1=bias_sum[:], scalar2=-1.0 / D, op0=ALU.add, op1=ALU.mult
+            )
+            nc.gpsimd.tensor_scalar(
+                out=yc_of[g][:, i, :],
+                in0=yc_of[g][:, i, :],
+                scalar1=1.0,
+                scalar2=neg_mean[:],
+                op0=ALU.mult,
+                op1=ALU.add,
+            )
+
+        def to_features(g, k):
+            if k == 0:
+                squares_of[g] = work.tile([P, NF, TG * P], F32, name="squares")
+                scaled_of[g] = work.tile([P, NF, TG * P], F32, name="scaled")
+            yct = psum_t.tile([P, 2, TG * P], F32, name="yct")
+            for jj in range(2):
+                feats = slice((2 * k + jj) * P, (2 * k + jj + 1) * P)
+                for i in range(TG):
+                    nc.tensor.transpose(yct[:, jj, i * P : (i + 1) * P], yc_of[g][:, i, feats], ident_f[:])
+            for jj in range(2):
+                j = 2 * k + jj
                 nc.scalar.activation(
-                    out=squares[:],
-                    in_=y[:, i, :],
+                    out=squares_of[g][:, j, :],
+                    in_=yct[:, jj, :],
                     func=ACT.Square,
-                    bias=neg_mean[:, i : i + 1],
+                    bias=bias_col[:, j : j + 1],
                     scale=1.0,
-                    accum_out=sq_sum[:],
                 )
-                std = small.tile([P, 1], F32, name="std")
-                nc.scalar.activation(out=std[:], in_=sq_sum[:], func=ACT.Sqrt, bias=eps[:], scale=1.0 / D)
-                rstd = small.tile([P, 1], F32, name="rstd")
-                nc.vector.reciprocal(out=rstd[:], in_=std[:])
-                o = work.tile([P, D], F32, name="o")
-                nc.vector.scalar_tensor_tensor(
-                    out=o[:], in0=y[:, i, :], scalar=neg_mean[:, i : i + 1], in1=gain_bc[:], op0=ALU.add, op1=ALU.mult
+                nc.scalar.activation(
+                    out=scaled_of[g][:, j, :],
+                    in_=yct[:, jj, :],
+                    func=ACT.Identity,
+                    bias=gain_bias_col[:, j : j + 1],
+                    scale=gain_col[:, j : j + 1],
                 )
-                nc.vector.scalar_tensor_tensor(
-                    out=o[:], in0=o[:], scalar=rstd[:], in1=shift_bc[:], op0=ALU.mult, op1=ALU.add
-                )
-                nc.sync.dma_start(out=out_view[:, g * T_PER_PASS + i, :], in_=o[:])
 
-        projected = [project(g) for g in range(NQ)]
-        for g in range(NQ):
-            y, chunk_sums = projected[g]
-            normalise(g, y, chunk_sums)
+        def add_squares(g, i, j_from, j_to):
+            if i == 0 and j_from == 0:
+                acc_of[g] = psum_v.tile([P, TG, P], F32, name="sq_acc")
+            for j in range(j_from, j_to):
+                nc.tensor.matmul(
+                    out=acc_of[g][:, i, :],
+                    lhsT=squares_of[g][:, j, i * P : (i + 1) * P],
+                    rhs=ident_f[:],
+                    is_transpose=True,
+                    start=(j == 0),
+                    stop=(j == NF - 1),
+                )
+
+        def finish_variance(g):
+            sq_sum = small.tile([P, TG], F32, name="sq_sum")
+            nc.vector.tensor_reduce(out=sq_sum[:], in_=acc_of[g][:], axis=AX.X, op=ALU.add)
+            std = small.tile([P, TG], F32, name="std")
+            nc.scalar.activation(out=std[:], in_=sq_sum[:], func=ACT.Sqrt, bias=eps[:], scale=1.0 / D)
+            rstd_of[g] = small.tile([P, TG], F32, name="rstd")
+            nc.vector.reciprocal(out=rstd_of[g][:], in_=std[:])
+
+        def to_tokens(g, i, c):
+            if i == 0 and c == 0:
+                o_of[g] = work.tile([P, TG, D], F32, name="o")
+            cols = slice(c * N_CHUNK, (c + 1) * N_CHUNK)
+            back = psum_n.tile([P, N_CHUNK], F32, name="back", tag="pn")
+            for jj in range(F_PER_CHUNK):
+                nc.tensor.transpose(
+                    back[:, jj * P : (jj + 1) * P],
+                    scaled_of[g][:, c * F_PER_CHUNK + jj, i * P : (i + 1) * P],
+                    ident_f[:],
+                )
+            nc.vector.scalar_tensor_tensor(
+                out=o_of[g][:, i, cols],
+                in0=back[:],
+                scalar=rstd_of[g][:, i : i + 1],
+                in1=shift_bc[:, cols],
+                op0=ALU.mult,
+                op1=ALU.add,
+            )
+            if i == TG - 1 and c == NC - 1:
+                nc.sync.dma_start(out=out_view[:, g * TG : (g + 1) * TG, :], in_=o_of[g][:])
+
+        STEPS = NF // 2
+        HALF = STEPS // 2
+        for g in range(-1, NG + 1):
+            for k in range(STEPS):
+                if 0 <= g < NG:
+                    to_features(g, k)
+                if g + 1 < NG and k < HALF:
+                    for n in (2 * k, 2 * k + 1):
+                        project(g + 1, n // NC, n % NC)
+                        if n % NC == NC - 1:
+                            centre(g + 1, n // NC)
+                if g >= 1 and k < HALF:
+                    add_squares(g - 1, k // 2, (k % 2) * (NF // 2), (k % 2 + 1) * (NF // 2))
+                    if k == HALF - 1:
+                        finish_variance(g - 1)
+                if g >= 1 and k >= HALF:
+                    for n in (2 * (k - HALF), 2 * (k - HALF) + 1):
+                        to_tokens(g - 1, n // NC, n % NC)

@@ -19,13 +19,13 @@ LQ = 1024
 D = 2048
 NT = LQ // P
 NF = D // P
-N_CHUNK = 512
-NC = D // N_CHUNK
-F_PER_CHUNK = N_CHUNK // P
+BANK = 512
+NC = D // BANK
+F_PER_CHUNK = BANK // P
 TG = 2
-NG = NT // TG
+PAIR = TG * P
+NP = NT // TG
 LN_EPS = 1e-5
-G_ROW = 32
 
 FLOPS = 2 * LQ * H * DV * D
 
@@ -34,35 +34,49 @@ def tile_multiheadattention_pb_kernel(tc, attn_out, residual, proj_w, proj_b, ln
     nc = tc.nc
     with ExitStack() as ctx:
         keep = ctx.enter_context(tc.tile_pool(name="keep", bufs=1))
-        work = ctx.enter_context(tc.tile_pool(name="work", bufs=2))
+        work = ctx.enter_context(tc.tile_pool(name="work", bufs=3))
         small = ctx.enter_context(tc.tile_pool(name="small", bufs=4))
-        psum_z = ctx.enter_context(tc.psum_pool(name="psum_z", bufs=2))
-        psum_t = ctx.enter_context(tc.psum_pool(name="psum_t", bufs=2))
-        psum_v = ctx.enter_context(tc.psum_pool(name="psum_v", bufs=1))
-        psum_n = ctx.enter_context(tc.psum_pool(name="psum_n", bufs=3))
+        psum_f = ctx.enter_context(tc.psum_pool(name="psum_f", bufs=4))
+        psum_t = ctx.enter_context(tc.psum_pool(name="psum_t", bufs=4))
 
-        vec_rows = keep.tile([P, P], BF16)
-        nc.vector.memset(vec_rows[:], 0.0)
-        nc.sync.dma_start(out=vec_rows[0:NF, :], in_=proj_b.rearrange("(j q) -> j q", q=P))
-        nc.sync.dma_start(out=vec_rows[G_ROW : G_ROW + NF, :], in_=ln_g.rearrange("(j q) -> j q", q=P))
+        bias_rows = keep.tile([P, P], BF16)
+        nc.vector.memset(bias_rows[:], 0.0)
+        nc.sync.dma_start(out=bias_rows[0:NF, :], in_=proj_b.rearrange("(j q) -> j q", q=P))
         x_raw = keep.tile([P, H, NT, DV], BF16)
-        nc.sync.dma_start(
-            out=x_raw[:].rearrange("p h t j -> p h (t j)"),
-            in_=attn_out.rearrange("h (p t) j -> p h (t j)", t=NT),
-        )
+        x_view = attn_out.rearrange("h (p t) j -> p h t j", t=NT)
         w_raw = keep.tile([P, H, D], BF16)
         w_view = proj_w.rearrange("(h q) n -> q h n", q=P)
-        for c in range(NC):
-            cols = slice(c * N_CHUNK, (c + 1) * N_CHUNK)
-            nc.sync.dma_start(out=w_raw[:, :, cols], in_=w_view[:, :, cols])
         r_sb = keep.tile([P, NT, D], BF16)
         r_view = residual.rearrange("(p t) n -> p t n", t=NT)
+        gain_bc = keep.tile([P, D], BF16)
         shift_bc = keep.tile([P, D], BF16)
-        for g in range(NG):
-            tiles = slice(g * TG, (g + 1) * TG)
+
+        def load_x(half):
+            tiles = slice(half * NT // 2, (half + 1) * NT // 2)
+            nc.sync.dma_start(
+                out=x_raw[:, :, tiles, :].rearrange("p h t j -> p h (t j)"),
+                in_=x_view[:, :, tiles, :].rearrange("p h t j -> p h (t j)"),
+            )
+
+        def load_w(c):
+            cols = slice(c * BANK, (c + 1) * BANK)
+            nc.sync.dma_start(out=w_raw[:, :, cols], in_=w_view[:, :, cols])
+
+        def load_r(pair):
+            tiles = slice(pair * TG, (pair + 1) * TG)
             nc.sync.dma_start(out=r_sb[:, tiles, :], in_=r_view[:, tiles, :])
-            if g == 1:
-                nc.sync.dma_start(out=shift_bc[:], in_=ln_b.partition_broadcast(P))
+
+        load_x(0)
+        load_w(0)
+        load_r(0)
+        for c in range(1, NC):
+            load_w(c)
+        load_r(1)
+        nc.sync.dma_start(out=gain_bc[:], in_=ln_g.partition_broadcast(P))
+        nc.sync.dma_start(out=shift_bc[:], in_=ln_b.partition_broadcast(P))
+        load_x(1)
+        for pair in range(2, NP):
+            load_r(pair)
 
         eps = keep.tile([P, 1], F32)
         nc.vector.memset(eps[:], LN_EPS)
@@ -72,44 +86,31 @@ def tile_multiheadattention_pb_kernel(tc, attn_out, residual, proj_w, proj_b, ln
         make_identity(nc, ident_b[:])
         ident_f = keep.tile([P, P], F32)
         make_identity(nc, ident_f[:])
-        ones_b = keep.tile([P, P], BF16)
-        nc.vector.memset(ones_b[:], 1.0)
-
-        vec_ps = psum_n.tile([P, P], BF16, tag="pn")
-        nc.tensor.transpose(vec_ps[:], vec_rows[:], ident_b[:])
-        vec_cols_b = keep.tile([P, P], BF16)
-        nc.vector.tensor_copy(out=vec_cols_b[:], in_=vec_ps[:])
-        vec_cols = keep.tile([P, P], F32)
-        nc.vector.tensor_copy(out=vec_cols[:], in_=vec_ps[:])
-        bias_col = vec_cols[:, 0:NF]
-        gain_col = vec_cols[:, G_ROW : G_ROW + NF]
-        gain_bias_col = keep.tile([P, NF], F32)
-        nc.vector.tensor_tensor(out=gain_bias_col[:], in0=gain_col, in1=bias_col, op=ALU.mult)
-        sum_ps = psum_n.tile([P, P], F32, tag="pn")
-        nc.tensor.matmul(out=sum_ps[:], lhsT=ones_b[:], rhs=vec_cols_b[:], start=True, stop=True)
-        bias_sum = keep.tile([P, 1], F32)
-        nc.vector.tensor_reduce(out=bias_sum[:], in_=sum_ps[:, 0:NF], axis=AX.X, op=ALU.add)
 
         x_grouped = keep.tile([P, NT, P, H], BF16, align_bytes=64)
         x_codes = keep.tile([P, NT * P], U32, align_bytes=64)
         x_scales = keep.tile([P, NT * P], U8, align_bytes=64)
-        for t in range(NT):
-            toks = slice(t * P, (t + 1) * P)
-            xt = psum_n.tile([P, H, P], BF16, tag="pn")
-            for h in range(H):
-                nc.tensor.transpose(xt[:, h, :], x_raw[:, h, t, :], ident_b[:])
-            nc.scalar.copy(out=x_grouped[:, t, :, :], in_=xt[:].rearrange("q h p -> q p h"))
-            nc.vector.quantize_mx(
-                out=x_codes[:, toks].bitcast(FP8X4),
-                scales=x_scales[:, toks],
-                in_=x_grouped[:, t, :, :].rearrange("q p h -> q (p h)"),
-            )
-
         w_grouped = keep.tile([P, D, H], BF16, align_bytes=64)
         w_codes = keep.tile([P, D], U32, align_bytes=64)
         w_scales = keep.tile([P, D], U8, align_bytes=64)
-        for c in range(NC):
-            cols = slice(c * N_CHUNK, (c + 1) * N_CHUNK)
+        bias_col = keep.tile([P, NF], F32)
+        out_view = out.rearrange("(p t) n -> p t n", t=NT)
+
+        def quantise_x(pair):
+            for t in range(pair * TG, (pair + 1) * TG):
+                xt = psum_t.tile([P, H, P], BF16, name="xt", tag="tok")
+                for h in range(H):
+                    nc.tensor.transpose(xt[:, h, :], x_raw[:, h, t, :], ident_b[:])
+                nc.scalar.copy(out=x_grouped[:, t, :, :], in_=xt[:].rearrange("q h p -> q p h"))
+            toks = slice(pair * PAIR, (pair + 1) * PAIR)
+            nc.vector.quantize_mx(
+                out=x_codes[:, toks].bitcast(FP8X4),
+                scales=x_scales[:, toks],
+                in_=x_grouped[:, pair * TG : (pair + 1) * TG, :, :].rearrange("q t p h -> q (t p h)"),
+            )
+
+        def quantise_w(c):
+            cols = slice(c * BANK, (c + 1) * BANK)
             w_rows = w_raw[:, :, cols].rearrange("q h n -> q n h")
             if c % 2 == 0:
                 nc.vector.tensor_copy(out=w_grouped[:, cols, :], in_=w_rows)
@@ -121,144 +122,112 @@ def tile_multiheadattention_pb_kernel(tc, attn_out, residual, proj_w, proj_b, ln
                 in_=w_grouped[:, cols, :].rearrange("q n h -> q (n h)"),
             )
 
-        out_view = out.rearrange("(p t) n -> p t n", t=NT)
-
-        yc_of = {}
+        y_of = {}
         sums_of = {}
-        squares_of = {}
-        scaled_of = {}
-        acc_of = {}
-        rstd_of = {}
+        zb_of = {}
+        neg_mean_of = {}
+        sq_sum_of = {}
         o_of = {}
 
-        def project(g, i, c):
-            if i == 0 and c == 0:
-                yc_of[g] = work.tile([P, TG, D], F32, name="yc")
+        def multiply(pair, c):
+            toks = slice(pair * PAIR, (pair + 1) * PAIR)
+            zb_of[pair, c] = work.tile([P, F_PER_CHUNK, PAIR], F32, name="zb")
+            for half in range(F_PER_CHUNK // 2):
+                z = psum_f.tile([P, 2, PAIR], F32, name="z")
+                for e in range(2):
+                    feats = slice((c * F_PER_CHUNK + 2 * half + e) * P, (c * F_PER_CHUNK + 2 * half + e + 1) * P)
+                    nc.tensor.matmul_mx(
+                        out=z[:, e, :],
+                        lhsT=w_codes[:, feats].bitcast(FP8X4),
+                        lhsT_scale=w_scales[:, feats],
+                        rhs=x_codes[:, toks].bitcast(FP8X4),
+                        rhs_scale=x_scales[:, toks],
+                        start=True,
+                        stop=True,
+                    )
+                for e in range(2):
+                    j = c * F_PER_CHUNK + 2 * half + e
+                    nc.scalar.activation(
+                        out=zb_of[pair, c][:, 2 * half + e, :],
+                        in_=z[:, e, :],
+                        func=ACT.Identity,
+                        bias=bias_col[:, j : j + 1],
+                        scale=1.0,
+                    )
+
+        def add_residual(pair, c):
             if c == 0:
-                sums_of[g, i] = small.tile([P, NC], F32, name="chunk_sums")
-            t = g * TG + i
-            toks = slice(t * P, (t + 1) * P)
-            cols = slice(c * N_CHUNK, (c + 1) * N_CHUNK)
-            z = psum_z.tile([P, N_CHUNK], F32, name="z")
-            nc.tensor.matmul_mx(
-                out=z[:],
-                lhsT=x_codes[:, toks].bitcast(FP8X4),
-                lhsT_scale=x_scales[:, toks],
-                rhs=w_codes[:, cols].bitcast(FP8X4),
-                rhs_scale=w_scales[:, cols],
-                start=True,
-                stop=True,
+                y_of[pair] = work.tile([P, TG, D], F32, name="y")
+                sums_of[pair] = small.tile([P, TG, NC], F32, name="chunk_sums")
+            cols = slice(c * BANK, (c + 1) * BANK)
+            for i in range(TG):
+                zbt = psum_t.tile([P, BANK], F32, name="zbt", tag="tok")
+                for jj in range(F_PER_CHUNK):
+                    nc.tensor.transpose(
+                        zbt[:, jj * P : (jj + 1) * P], zb_of[pair, c][:, jj, i * P : (i + 1) * P], ident_f[:]
+                    )
+                nc.vector.scalar_tensor_tensor(
+                    out=y_of[pair][:, i, cols],
+                    in0=zbt[:],
+                    scalar=0.0,
+                    in1=r_sb[:, pair * TG + i, cols],
+                    op0=ALU.add,
+                    op1=ALU.add,
+                    accum_out=sums_of[pair][:, i, c : c + 1],
+                )
+            if c == NC - 1:
+                row_sum = small.tile([P, TG], F32, name="row_sum")
+                nc.vector.tensor_reduce(out=row_sum[:], in_=sums_of[pair][:], axis=AX.X, op=ALU.add)
+                neg_mean_of[pair] = small.tile([P, TG], F32, name="neg_mean")
+                nc.vector.tensor_scalar_mul(out=neg_mean_of[pair][:], in0=row_sum[:], scalar1=-1.0 / D)
+
+        def centre_and_gain(pair, i):
+            neg_mean = neg_mean_of[pair][:, i : i + 1]
+            squares = work.tile([P, D], BF16, name="squares")
+            sq_sum_of[pair, i] = small.tile([P, 1], F32, name="sq_sum")
+            nc.scalar.activation(
+                out=squares[:],
+                in_=y_of[pair][:, i, :],
+                func=ACT.Square,
+                bias=neg_mean,
+                scale=1.0,
+                accum_out=sq_sum_of[pair, i][:],
             )
+            o_of[pair, i] = work.tile([P, D], F32, name="o")
             nc.vector.scalar_tensor_tensor(
-                out=yc_of[g][:, i, cols],
-                in0=z[:],
-                scalar=0.0,
-                in1=r_sb[:, t, cols],
-                op0=ALU.add,
-                op1=ALU.add,
-                accum_out=sums_of[g, i][:, c : c + 1],
+                out=o_of[pair, i][:], in0=y_of[pair][:, i, :], scalar=neg_mean, in1=gain_bc[:], op0=ALU.add, op1=ALU.mult
             )
 
-        def centre(g, i):
-            row_sum = small.tile([P, 1], F32, name="row_sum")
-            nc.vector.tensor_reduce(out=row_sum[:], in_=sums_of[g, i][:], axis=AX.X, op=ALU.add)
-            neg_mean = small.tile([P, 1], F32, name="neg_mean")
-            nc.vector.tensor_scalar(
-                out=neg_mean[:], in0=row_sum[:], scalar1=bias_sum[:], scalar2=-1.0 / D, op0=ALU.add, op1=ALU.mult
-            )
-            nc.gpsimd.tensor_scalar(
-                out=yc_of[g][:, i, :],
-                in0=yc_of[g][:, i, :],
-                scalar1=1.0,
-                scalar2=neg_mean[:],
-                op0=ALU.mult,
-                op1=ALU.add,
-            )
-
-        def to_features(g, k):
-            if k == 0:
-                squares_of[g] = work.tile([P, NF, TG * P], F32, name="squares")
-                scaled_of[g] = work.tile([P, NF, TG * P], F32, name="scaled")
-            yct = psum_t.tile([P, 2, TG * P], F32, name="yct")
-            for jj in range(2):
-                feats = slice((2 * k + jj) * P, (2 * k + jj + 1) * P)
-                for i in range(TG):
-                    nc.tensor.transpose(yct[:, jj, i * P : (i + 1) * P], yc_of[g][:, i, feats], ident_f[:])
-            for jj in range(2):
-                j = 2 * k + jj
-                nc.scalar.activation(
-                    out=squares_of[g][:, j, :],
-                    in_=yct[:, jj, :],
-                    func=ACT.Square,
-                    bias=bias_col[:, j : j + 1],
-                    scale=1.0,
-                )
-                nc.scalar.activation(
-                    out=scaled_of[g][:, j, :],
-                    in_=yct[:, jj, :],
-                    func=ACT.Identity,
-                    bias=gain_bias_col[:, j : j + 1],
-                    scale=gain_col[:, j : j + 1],
-                )
-
-        def add_squares(g, i, j_from, j_to):
-            if i == 0 and j_from == 0:
-                acc_of[g] = psum_v.tile([P, TG, P], F32, name="sq_acc")
-            for j in range(j_from, j_to):
-                nc.tensor.matmul(
-                    out=acc_of[g][:, i, :],
-                    lhsT=squares_of[g][:, j, i * P : (i + 1) * P],
-                    rhs=ident_f[:],
-                    is_transpose=True,
-                    start=(j == 0),
-                    stop=(j == NF - 1),
-                )
-
-        def finish_variance(g):
-            sq_sum = small.tile([P, TG], F32, name="sq_sum")
-            nc.vector.tensor_reduce(out=sq_sum[:], in_=acc_of[g][:], axis=AX.X, op=ALU.add)
-            std = small.tile([P, TG], F32, name="std")
-            nc.scalar.activation(out=std[:], in_=sq_sum[:], func=ACT.Sqrt, bias=eps[:], scale=1.0 / D)
-            rstd_of[g] = small.tile([P, TG], F32, name="rstd")
-            nc.vector.reciprocal(out=rstd_of[g][:], in_=std[:])
-
-        def to_tokens(g, i, c):
-            if i == 0 and c == 0:
-                o_of[g] = work.tile([P, TG, D], F32, name="o")
-            cols = slice(c * N_CHUNK, (c + 1) * N_CHUNK)
-            back = psum_n.tile([P, N_CHUNK], F32, name="back", tag="pn")
-            for jj in range(F_PER_CHUNK):
-                nc.tensor.transpose(
-                    back[:, jj * P : (jj + 1) * P],
-                    scaled_of[g][:, c * F_PER_CHUNK + jj, i * P : (i + 1) * P],
-                    ident_f[:],
-                )
+        def scale_and_shift(pair, i):
+            std = small.tile([P, 1], F32, name="std")
+            nc.scalar.activation(out=std[:], in_=sq_sum_of[pair, i][:], func=ACT.Sqrt, bias=eps[:], scale=1.0 / D)
+            rstd = small.tile([P, 1], F32, name="rstd")
+            nc.vector.reciprocal(out=rstd[:], in_=std[:])
             nc.vector.scalar_tensor_tensor(
-                out=o_of[g][:, i, cols],
-                in0=back[:],
-                scalar=rstd_of[g][:, i : i + 1],
-                in1=shift_bc[:, cols],
-                op0=ALU.mult,
-                op1=ALU.add,
+                out=o_of[pair, i][:], in0=o_of[pair, i][:], scalar=rstd[:], in1=shift_bc[:], op0=ALU.mult, op1=ALU.add
             )
-            if i == TG - 1 and c == NC - 1:
-                nc.sync.dma_start(out=out_view[:, g * TG : (g + 1) * TG, :], in_=o_of[g][:])
+            nc.sync.dma_start(out=out_view[:, pair * TG + i, :], in_=o_of[pair, i][:])
 
-        STEPS = NF // 2
-        HALF = STEPS // 2
-        for g in range(-1, NG + 1):
-            for k in range(STEPS):
-                if 0 <= g < NG:
-                    to_features(g, k)
-                if g + 1 < NG and k < HALF:
-                    for n in (2 * k, 2 * k + 1):
-                        project(g + 1, n // NC, n % NC)
-                        if n % NC == NC - 1:
-                            centre(g + 1, n // NC)
-                if g >= 1 and k < HALF:
-                    add_squares(g - 1, k // 2, (k % 2) * (NF // 2), (k % 2 + 1) * (NF // 2))
-                    if k == HALF - 1:
-                        finish_variance(g - 1)
-                if g >= 1 and k >= HALF:
-                    for n in (2 * (k - HALF), 2 * (k - HALF) + 1):
-                        to_tokens(g - 1, n // NC, n % NC)
+        quantise_x(0)
+        bias_ps = psum_t.tile([P, P], BF16, tag="tok")
+        nc.tensor.transpose(bias_ps[:], bias_rows[:], ident_b[:])
+        nc.vector.tensor_copy(out=bias_col[:], in_=bias_ps[:, 0:NF])
+        quantise_w(0)
+        multiply(0, 0)
+        quantise_x(1)
+        for pair in range(NP + 1):
+            for c in range(NC):
+                if pair == 0 and c + 1 < NC:
+                    quantise_w(c + 1)
+                if pair + 2 < NP and c == 0:
+                    quantise_x(pair + 2)
+                if c + 1 < NC and pair < NP:
+                    multiply(pair, c + 1)
+                if c + 1 == NC and pair + 1 < NP:
+                    multiply(pair + 1, 0)
+                if pair < NP:
+                    add_residual(pair, c)
+                if pair >= 1 and c < TG:
+                    centre_and_gain(pair - 1, c)
+                if pair >= 1 and c >= TG:
+                    scale_and_shift(pair - 1, c - TG)

@@ -26,6 +26,7 @@ TG = 2
 PAIR = TG * P
 NP = NT // TG
 LN_EPS = 1e-5
+BIAS_ROW, GAIN_ROW, SHIFT_ROW = 0, 32, 64
 
 FLOPS = 2 * LQ * H * DV * D
 
@@ -39,9 +40,10 @@ def tile_multiheadattention_pb_kernel(tc, attn_out, residual, proj_w, proj_b, ln
         psum_f = ctx.enter_context(tc.psum_pool(name="psum_f", bufs=4))
         psum_t = ctx.enter_context(tc.psum_pool(name="psum_t", bufs=4))
 
-        bias_rows = keep.tile([P, P], BF16)
-        nc.vector.memset(bias_rows[:], 0.0)
-        nc.sync.dma_start(out=bias_rows[0:NF, :], in_=proj_b.rearrange("(j q) -> j q", q=P))
+        vec_rows = keep.tile([P, P], BF16)
+        nc.vector.memset(vec_rows[:], 0.0)
+        for row, vec in ((BIAS_ROW, proj_b), (GAIN_ROW, ln_g), (SHIFT_ROW, ln_b)):
+            nc.sync.dma_start(out=vec_rows[row : row + NF, :], in_=vec.rearrange("(j q) -> j q", q=P))
         x_raw = keep.tile([P, H, NT, DV], BF16)
         x_view = attn_out.rearrange("h (p t) j -> p h t j", t=NT)
         w_raw = keep.tile([P, H, D], BF16)
@@ -72,8 +74,6 @@ def tile_multiheadattention_pb_kernel(tc, attn_out, residual, proj_w, proj_b, ln
         for c in range(1, NC):
             load_w(c)
         load_r(1)
-        nc.sync.dma_start(out=gain_bc[:], in_=ln_g.partition_broadcast(P))
-        nc.sync.dma_start(out=shift_bc[:], in_=ln_b.partition_broadcast(P))
         load_x(1)
         for pair in range(2, NP):
             load_r(pair)
@@ -93,7 +93,8 @@ def tile_multiheadattention_pb_kernel(tc, attn_out, residual, proj_w, proj_b, ln
         w_grouped = keep.tile([P, D, H], BF16, align_bytes=64)
         w_codes = keep.tile([P, D], U32, align_bytes=64)
         w_scales = keep.tile([P, D], U8, align_bytes=64)
-        bias_col = keep.tile([P, NF], F32)
+        vec_cols = keep.tile([P, P], F32)
+        bias_col = vec_cols[:, BIAS_ROW : BIAS_ROW + NF]
         out_view = out.rearrange("(p t) n -> p t n", t=NT)
 
         def quantise_x(pair):
@@ -121,6 +122,16 @@ def tile_multiheadattention_pb_kernel(tc, attn_out, residual, proj_w, proj_b, ln
                 scales=w_scales[:, cols],
                 in_=w_grouped[:, cols, :].rearrange("q n h -> q (n h)"),
             )
+
+        def spread(row, everywhere):
+            for c in range(NC):
+                rows_ps = psum_t.tile([P, BANK], F32, name="rows_ps", tag="tok")
+                for jj in range(F_PER_CHUNK):
+                    col = row + c * F_PER_CHUNK + jj
+                    nc.tensor.transpose(
+                        rows_ps[:, jj * P : (jj + 1) * P], vec_cols[:, col : col + 1].to_broadcast([P, P]), ident_f[:]
+                    )
+                nc.scalar.copy(out=everywhere[:, c * BANK : (c + 1) * BANK], in_=rows_ps[:])
 
         y_of = {}
         sums_of = {}
@@ -209,12 +220,14 @@ def tile_multiheadattention_pb_kernel(tc, attn_out, residual, proj_w, proj_b, ln
             nc.sync.dma_start(out=out_view[:, pair * TG + i, :], in_=o_of[pair, i][:])
 
         quantise_x(0)
-        bias_ps = psum_t.tile([P, P], BF16, tag="tok")
-        nc.tensor.transpose(bias_ps[:], bias_rows[:], ident_b[:])
-        nc.vector.tensor_copy(out=bias_col[:], in_=bias_ps[:, 0:NF])
+        vec_ps = psum_t.tile([P, P], BF16, tag="tok")
+        nc.tensor.transpose(vec_ps[:], vec_rows[:], ident_b[:])
+        nc.vector.tensor_copy(out=vec_cols[:], in_=vec_ps[:])
         quantise_w(0)
         multiply(0, 0)
         quantise_x(1)
+        spread(GAIN_ROW, gain_bc)
+        spread(SHIFT_ROW, shift_bc)
         for pair in range(NP + 1):
             for c in range(NC):
                 if pair == 0 and c + 1 < NC:

@@ -22,11 +22,9 @@ NF = D // P
 BANK = 512
 NC = D // BANK
 F_PER_CHUNK = BANK // P
-TG = 2
-PAIR = TG * P
-NP = NT // TG
+TG = BANK // P
+NG = NT // TG
 LN_EPS = 1e-5
-BIAS_ROW, GAIN_ROW, SHIFT_ROW = 0, 32, 64
 
 FLOPS = 2 * LQ * H * DV * D
 
@@ -35,15 +33,15 @@ def tile_multiheadattention_pb_kernel(tc, attn_out, residual, proj_w, proj_b, ln
     nc = tc.nc
     with ExitStack() as ctx:
         keep = ctx.enter_context(tc.tile_pool(name="keep", bufs=1))
+        rows = ctx.enter_context(tc.tile_pool(name="rows", bufs=NG))
         work = ctx.enter_context(tc.tile_pool(name="work", bufs=3))
         small = ctx.enter_context(tc.tile_pool(name="small", bufs=4))
         psum_f = ctx.enter_context(tc.psum_pool(name="psum_f", bufs=4))
         psum_t = ctx.enter_context(tc.psum_pool(name="psum_t", bufs=4))
 
-        vec_rows = keep.tile([P, P], BF16)
-        nc.vector.memset(vec_rows[:], 0.0)
-        for row, vec in ((BIAS_ROW, proj_b), (GAIN_ROW, ln_g), (SHIFT_ROW, ln_b)):
-            nc.sync.dma_start(out=vec_rows[row : row + NF, :], in_=vec.rearrange("(j q) -> j q", q=P))
+        bias_rows = keep.tile([P, P], BF16)
+        nc.vector.memset(bias_rows[:], 0.0)
+        nc.sync.dma_start(out=bias_rows[0:NF, :], in_=proj_b.rearrange("(j q) -> j q", q=P))
         x_raw = keep.tile([P, H, NT, DV], BF16)
         x_view = attn_out.rearrange("h (p t) j -> p h t j", t=NT)
         w_raw = keep.tile([P, H, D], BF16)
@@ -53,8 +51,8 @@ def tile_multiheadattention_pb_kernel(tc, attn_out, residual, proj_w, proj_b, ln
         gain_bc = keep.tile([P, D], BF16)
         shift_bc = keep.tile([P, D], BF16)
 
-        def load_x(half):
-            tiles = slice(half * NT // 2, (half + 1) * NT // 2)
+        def load_x(g):
+            tiles = slice(g * TG, (g + 1) * TG)
             nc.sync.dma_start(
                 out=x_raw[:, :, tiles, :].rearrange("p h t j -> p h (t j)"),
                 in_=x_view[:, :, tiles, :].rearrange("p h t j -> p h (t j)"),
@@ -64,19 +62,21 @@ def tile_multiheadattention_pb_kernel(tc, attn_out, residual, proj_w, proj_b, ln
             cols = slice(c * BANK, (c + 1) * BANK)
             nc.sync.dma_start(out=w_raw[:, :, cols], in_=w_view[:, :, cols])
 
-        def load_r(pair):
-            tiles = slice(pair * TG, (pair + 1) * TG)
-            nc.sync.dma_start(out=r_sb[:, tiles, :], in_=r_view[:, tiles, :])
+        def load_r(g, c):
+            tiles = slice(g * TG, (g + 1) * TG)
+            cols = slice(c * BANK, (c + 1) * BANK)
+            nc.sync.dma_start(out=r_sb[:, tiles, cols], in_=r_view[:, tiles, cols])
 
         load_x(0)
-        load_w(0)
-        load_r(0)
-        for c in range(1, NC):
+        for c in range(NC):
             load_w(c)
-        load_r(1)
+            load_r(0, c)
         load_x(1)
-        for pair in range(2, NP):
-            load_r(pair)
+        nc.sync.dma_start(out=gain_bc[:], in_=ln_g.partition_broadcast(P))
+        load_r(1, 0)
+        nc.sync.dma_start(out=shift_bc[:], in_=ln_b.partition_broadcast(P))
+        for c in range(1, NC):
+            load_r(1, c)
 
         eps = keep.tile([P, 1], F32)
         nc.vector.memset(eps[:], LN_EPS)
@@ -93,21 +93,20 @@ def tile_multiheadattention_pb_kernel(tc, attn_out, residual, proj_w, proj_b, ln
         w_grouped = keep.tile([P, D, H], BF16, align_bytes=64)
         w_codes = keep.tile([P, D], U32, align_bytes=64)
         w_scales = keep.tile([P, D], U8, align_bytes=64)
-        vec_cols = keep.tile([P, P], F32)
-        bias_col = vec_cols[:, BIAS_ROW : BIAS_ROW + NF]
+        bias_col = keep.tile([P, NF], F32)
         out_view = out.rearrange("(p t) n -> p t n", t=NT)
 
-        def quantise_x(pair):
-            for t in range(pair * TG, (pair + 1) * TG):
+        def quantise_x(g):
+            for t in range(g * TG, (g + 1) * TG):
                 xt = psum_t.tile([P, H, P], BF16, name="xt", tag="tok")
                 for h in range(H):
                     nc.tensor.transpose(xt[:, h, :], x_raw[:, h, t, :], ident_b[:])
                 nc.scalar.copy(out=x_grouped[:, t, :, :], in_=xt[:].rearrange("q h p -> q p h"))
-            toks = slice(pair * PAIR, (pair + 1) * PAIR)
+            toks = slice(g * BANK, (g + 1) * BANK)
             nc.vector.quantize_mx(
                 out=x_codes[:, toks].bitcast(FP8X4),
                 scales=x_scales[:, toks],
-                in_=x_grouped[:, pair * TG : (pair + 1) * TG, :, :].rearrange("q t p h -> q (t p h)"),
+                in_=x_grouped[:, g * TG : (g + 1) * TG, :, :].rearrange("q t p h -> q (t p h)"),
             )
 
         def quantise_w(c):
@@ -123,124 +122,92 @@ def tile_multiheadattention_pb_kernel(tc, attn_out, residual, proj_w, proj_b, ln
                 in_=w_grouped[:, cols, :].rearrange("q n h -> q (n h)"),
             )
 
-        def spread(row, everywhere):
-            for c in range(NC):
-                rows_ps = psum_t.tile([P, BANK], F32, name="rows_ps", tag="tok")
-                for jj in range(F_PER_CHUNK):
-                    col = row + c * F_PER_CHUNK + jj
-                    nc.tensor.transpose(
-                        rows_ps[:, jj * P : (jj + 1) * P], vec_cols[:, col : col + 1].to_broadcast([P, P]), ident_f[:]
-                    )
-                nc.scalar.copy(out=everywhere[:, c * BANK : (c + 1) * BANK], in_=rows_ps[:])
-
         y_of = {}
         sums_of = {}
         zb_of = {}
         neg_mean_of = {}
-        sq_sum_of = {}
-        o_of = {}
 
-        def multiply(pair, c):
-            toks = slice(pair * PAIR, (pair + 1) * PAIR)
-            zb_of[pair, c] = work.tile([P, F_PER_CHUNK, PAIR], F32, name="zb")
-            for half in range(F_PER_CHUNK // 2):
-                z = psum_f.tile([P, 2, PAIR], F32, name="z")
-                for e in range(2):
-                    feats = slice((c * F_PER_CHUNK + 2 * half + e) * P, (c * F_PER_CHUNK + 2 * half + e + 1) * P)
-                    nc.tensor.matmul_mx(
-                        out=z[:, e, :],
-                        lhsT=w_codes[:, feats].bitcast(FP8X4),
-                        lhsT_scale=w_scales[:, feats],
-                        rhs=x_codes[:, toks].bitcast(FP8X4),
-                        rhs_scale=x_scales[:, toks],
-                        start=True,
-                        stop=True,
-                    )
-                for e in range(2):
-                    j = c * F_PER_CHUNK + 2 * half + e
-                    nc.scalar.activation(
-                        out=zb_of[pair, c][:, 2 * half + e, :],
-                        in_=z[:, e, :],
-                        func=ACT.Identity,
-                        bias=bias_col[:, j : j + 1],
-                        scale=1.0,
-                    )
+        def multiply(g, c):
+            toks = slice(g * BANK, (g + 1) * BANK)
+            zb_of[g, c] = work.tile([P, F_PER_CHUNK, BANK], F32, name="zb")
+            for jj in range(F_PER_CHUNK):
+                j = c * F_PER_CHUNK + jj
+                feats = slice(j * P, (j + 1) * P)
+                z = psum_f.tile([P, BANK], F32, name="z")
+                nc.tensor.matmul_mx(
+                    out=z[:],
+                    lhsT=w_codes[:, feats].bitcast(FP8X4),
+                    lhsT_scale=w_scales[:, feats],
+                    rhs=x_codes[:, toks].bitcast(FP8X4),
+                    rhs_scale=x_scales[:, toks],
+                    start=True,
+                    stop=True,
+                )
+                nc.scalar.activation(
+                    out=zb_of[g, c][:, jj, :], in_=z[:], func=ACT.Identity, bias=bias_col[:, j : j + 1], scale=1.0
+                )
 
-        def add_residual(pair, c):
+        def add_residual(g, c):
             if c == 0:
-                y_of[pair] = work.tile([P, TG, D], F32, name="y")
-                sums_of[pair] = small.tile([P, TG, NC], F32, name="chunk_sums")
+                y_of[g] = rows.tile([P, TG, D], F32, name="y")
+                sums_of[g] = small.tile([P, TG, NC], F32, name="chunk_sums")
             cols = slice(c * BANK, (c + 1) * BANK)
             for i in range(TG):
                 zbt = psum_t.tile([P, BANK], F32, name="zbt", tag="tok")
                 for jj in range(F_PER_CHUNK):
-                    nc.tensor.transpose(
-                        zbt[:, jj * P : (jj + 1) * P], zb_of[pair, c][:, jj, i * P : (i + 1) * P], ident_f[:]
-                    )
+                    nc.tensor.transpose(zbt[:, jj * P : (jj + 1) * P], zb_of[g, c][:, jj, i * P : (i + 1) * P], ident_f[:])
                 nc.vector.scalar_tensor_tensor(
-                    out=y_of[pair][:, i, cols],
+                    out=y_of[g][:, i, cols],
                     in0=zbt[:],
                     scalar=0.0,
-                    in1=r_sb[:, pair * TG + i, cols],
+                    in1=r_sb[:, g * TG + i, cols],
                     op0=ALU.add,
                     op1=ALU.add,
-                    accum_out=sums_of[pair][:, i, c : c + 1],
+                    accum_out=sums_of[g][:, i, c : c + 1],
                 )
             if c == NC - 1:
                 row_sum = small.tile([P, TG], F32, name="row_sum")
-                nc.vector.tensor_reduce(out=row_sum[:], in_=sums_of[pair][:], axis=AX.X, op=ALU.add)
-                neg_mean_of[pair] = small.tile([P, TG], F32, name="neg_mean")
-                nc.vector.tensor_scalar_mul(out=neg_mean_of[pair][:], in0=row_sum[:], scalar1=-1.0 / D)
+                nc.vector.tensor_reduce(out=row_sum[:], in_=sums_of[g][:], axis=AX.X, op=ALU.add)
+                neg_mean_of[g] = small.tile([P, TG], F32, name="neg_mean")
+                nc.vector.tensor_scalar_mul(out=neg_mean_of[g][:], in0=row_sum[:], scalar1=-1.0 / D)
 
-        def centre_and_gain(pair, i):
-            neg_mean = neg_mean_of[pair][:, i : i + 1]
+        def normalise(g, i):
+            neg_mean = neg_mean_of[g][:, i : i + 1]
             squares = work.tile([P, D], BF16, name="squares")
-            sq_sum_of[pair, i] = small.tile([P, 1], F32, name="sq_sum")
+            sq_sum = small.tile([P, 1], F32, name="sq_sum")
             nc.scalar.activation(
-                out=squares[:],
-                in_=y_of[pair][:, i, :],
-                func=ACT.Square,
-                bias=neg_mean,
-                scale=1.0,
-                accum_out=sq_sum_of[pair, i][:],
+                out=squares[:], in_=y_of[g][:, i, :], func=ACT.Square, bias=neg_mean, scale=1.0, accum_out=sq_sum[:]
             )
-            o_of[pair, i] = work.tile([P, D], F32, name="o")
-            nc.vector.scalar_tensor_tensor(
-                out=o_of[pair, i][:], in0=y_of[pair][:, i, :], scalar=neg_mean, in1=gain_bc[:], op0=ALU.add, op1=ALU.mult
-            )
-
-        def scale_and_shift(pair, i):
             std = small.tile([P, 1], F32, name="std")
-            nc.scalar.activation(out=std[:], in_=sq_sum_of[pair, i][:], func=ACT.Sqrt, bias=eps[:], scale=1.0 / D)
+            nc.scalar.activation(out=std[:], in_=sq_sum[:], func=ACT.Sqrt, bias=eps[:], scale=1.0 / D)
+            o = work.tile([P, D], F32, name="o")
+            nc.vector.scalar_tensor_tensor(
+                out=o[:], in0=y_of[g][:, i, :], scalar=neg_mean, in1=gain_bc[:], op0=ALU.add, op1=ALU.mult
+            )
             rstd = small.tile([P, 1], F32, name="rstd")
             nc.vector.reciprocal(out=rstd[:], in_=std[:])
             nc.vector.scalar_tensor_tensor(
-                out=o_of[pair, i][:], in0=o_of[pair, i][:], scalar=rstd[:], in1=shift_bc[:], op0=ALU.mult, op1=ALU.add
+                out=o[:], in0=o[:], scalar=rstd[:], in1=shift_bc[:], op0=ALU.mult, op1=ALU.add
             )
-            nc.sync.dma_start(out=out_view[:, pair * TG + i, :], in_=o_of[pair, i][:])
+            nc.sync.dma_start(out=out_view[:, g * TG + i, :], in_=o[:])
 
         quantise_x(0)
-        vec_ps = psum_t.tile([P, P], BF16, tag="tok")
-        nc.tensor.transpose(vec_ps[:], vec_rows[:], ident_b[:])
-        nc.vector.tensor_copy(out=vec_cols[:], in_=vec_ps[:])
+        bias_ps = psum_t.tile([P, P], BF16, tag="tok")
+        nc.tensor.transpose(bias_ps[:], bias_rows[:], ident_b[:])
+        nc.vector.tensor_copy(out=bias_col[:], in_=bias_ps[:, 0:NF])
         quantise_w(0)
         multiply(0, 0)
-        quantise_x(1)
-        spread(GAIN_ROW, gain_bc)
-        spread(SHIFT_ROW, shift_bc)
-        for pair in range(NP + 1):
+        for g in range(NG + 1):
             for c in range(NC):
-                if pair == 0 and c + 1 < NC:
+                if g == 0 and c + 1 < NC:
                     quantise_w(c + 1)
-                if pair + 2 < NP and c == 0:
-                    quantise_x(pair + 2)
-                if c + 1 < NC and pair < NP:
-                    multiply(pair, c + 1)
-                if c + 1 == NC and pair + 1 < NP:
-                    multiply(pair + 1, 0)
-                if pair < NP:
-                    add_residual(pair, c)
-                if pair >= 1 and c < TG:
-                    centre_and_gain(pair - 1, c)
-                if pair >= 1 and c >= TG:
-                    scale_and_shift(pair - 1, c - TG)
+                if g + 1 < NG and c == 0:
+                    quantise_x(g + 1)
+                if c + 1 < NC and g < NG:
+                    multiply(g, c + 1)
+                if c + 1 == NC and g + 1 < NG:
+                    multiply(g + 1, 0)
+                if g < NG:
+                    add_residual(g, c)
+                if g >= 1:
+                    normalise(g - 1, c)

from contextlib import ExitStack

import concourse.mybir as mybir
from concourse.masks import make_identity

F32 = mybir.dt.float32
BF16 = mybir.dt.bfloat16
U32 = mybir.dt.uint32
U8 = mybir.dt.uint8
FP8X4 = mybir.dt.float8_e4m3fn_x4
ALU = mybir.AluOpType
ACT = mybir.ActivationFunctionType
AX = mybir.AxisListType

P = 128
H = 4
DV = 128
LQ = 1024
D = 2048
NT = LQ // P
NF = D // P
BANK = 512
NC = D // BANK
F_PER_CHUNK = BANK // P
TG = BANK // P
NG = NT // TG
LN_EPS = 1e-5

FLOPS = 2 * LQ * H * DV * D


def tile_multiheadattention_pb_kernel(tc, attn_out, residual, proj_w, proj_b, ln_g, ln_b, out):
    nc = tc.nc
    with ExitStack() as ctx:
        keep = ctx.enter_context(tc.tile_pool(name="keep", bufs=1))
        rows = ctx.enter_context(tc.tile_pool(name="rows", bufs=NG))
        work = ctx.enter_context(tc.tile_pool(name="work", bufs=3))
        small = ctx.enter_context(tc.tile_pool(name="small", bufs=4))
        psum_f = ctx.enter_context(tc.psum_pool(name="psum_f", bufs=4))
        psum_t = ctx.enter_context(tc.psum_pool(name="psum_t", bufs=4))

        bias_rows = keep.tile([P, P], BF16)
        nc.vector.memset(bias_rows[:], 0.0)
        nc.sync.dma_start(out=bias_rows[0:NF, :], in_=proj_b.rearrange("(j q) -> j q", q=P))
        x_raw = keep.tile([P, H, NT, DV], BF16)
        x_view = attn_out.rearrange("h (p t) j -> p h t j", t=NT)
        w_raw = keep.tile([P, H, D], BF16)
        w_view = proj_w.rearrange("(h q) n -> q h n", q=P)
        r_sb = keep.tile([P, NT, D], BF16)
        r_view = residual.rearrange("(p t) n -> p t n", t=NT)
        gain_bc = keep.tile([P, D], BF16)
        shift_bc = keep.tile([P, D], BF16)

        def load_x(g):
            tiles = slice(g * TG, (g + 1) * TG)
            nc.sync.dma_start(
                out=x_raw[:, :, tiles, :].rearrange("p h t j -> p h (t j)"),
                in_=x_view[:, :, tiles, :].rearrange("p h t j -> p h (t j)"),
            )

        def load_w(c):
            cols = slice(c * BANK, (c + 1) * BANK)
            nc.sync.dma_start(out=w_raw[:, :, cols], in_=w_view[:, :, cols])

        def load_r(g, c):
            tiles = slice(g * TG, (g + 1) * TG)
            cols = slice(c * BANK, (c + 1) * BANK)
            nc.sync.dma_start(out=r_sb[:, tiles, cols], in_=r_view[:, tiles, cols])

        load_x(0)
        for c in range(NC):
            load_w(c)
            load_r(0, c)
        load_x(1)
        nc.sync.dma_start(out=gain_bc[:], in_=ln_g.partition_broadcast(P))
        load_r(1, 0)
        nc.sync.dma_start(out=shift_bc[:], in_=ln_b.partition_broadcast(P))
        for c in range(1, NC):
            load_r(1, c)

        eps = keep.tile([P, 1], F32)
        nc.vector.memset(eps[:], LN_EPS)
        warm = keep.tile([P, 1], F32)
        nc.scalar.activation(out=warm[:], in_=eps[:], func=ACT.Sqrt)
        ident_b = keep.tile([P, P], BF16)
        make_identity(nc, ident_b[:])
        ident_f = keep.tile([P, P], F32)
        make_identity(nc, ident_f[:])

        x_grouped = keep.tile([P, NT, P, H], BF16, align_bytes=64)
        x_codes = keep.tile([P, NT * P], U32, align_bytes=64)
        x_scales = keep.tile([P, NT * P], U8, align_bytes=64)
        w_grouped = keep.tile([P, D, H], BF16, align_bytes=64)
        w_codes = keep.tile([P, D], U32, align_bytes=64)
        w_scales = keep.tile([P, D], U8, align_bytes=64)
        bias_col = keep.tile([P, NF], F32)
        out_view = out.rearrange("(p t) n -> p t n", t=NT)

        def quantise_x(g):
            for t in range(g * TG, (g + 1) * TG):
                xt = psum_t.tile([P, H, P], BF16, name="xt", tag="tok")
                for h in range(H):
                    nc.tensor.transpose(xt[:, h, :], x_raw[:, h, t, :], ident_b[:])
                nc.scalar.copy(out=x_grouped[:, t, :, :], in_=xt[:].rearrange("q h p -> q p h"))
            toks = slice(g * BANK, (g + 1) * BANK)
            nc.vector.quantize_mx(
                out=x_codes[:, toks].bitcast(FP8X4),
                scales=x_scales[:, toks],
                in_=x_grouped[:, g * TG : (g + 1) * TG, :, :].rearrange("q t p h -> q (t p h)"),
            )

        def quantise_w(c):
            cols = slice(c * BANK, (c + 1) * BANK)
            w_rows = w_raw[:, :, cols].rearrange("q h n -> q n h")
            if c % 2 == 0:
                nc.vector.tensor_copy(out=w_grouped[:, cols, :], in_=w_rows)
            else:
                nc.scalar.copy(out=w_grouped[:, cols, :], in_=w_rows)
            nc.vector.quantize_mx(
                out=w_codes[:, cols].bitcast(FP8X4),
                scales=w_scales[:, cols],
                in_=w_grouped[:, cols, :].rearrange("q n h -> q (n h)"),
            )

        y_of = {}
        sums_of = {}
        zb_of = {}
        neg_mean_of = {}

        def multiply(g, c):
            toks = slice(g * BANK, (g + 1) * BANK)
            zb_of[g, c] = work.tile([P, F_PER_CHUNK, BANK], F32, name="zb")
            for jj in range(F_PER_CHUNK):
                j = c * F_PER_CHUNK + jj
                feats = slice(j * P, (j + 1) * P)
                z = psum_f.tile([P, BANK], F32, name="z")
                nc.tensor.matmul_mx(
                    out=z[:],
                    lhsT=w_codes[:, feats].bitcast(FP8X4),
                    lhsT_scale=w_scales[:, feats],
                    rhs=x_codes[:, toks].bitcast(FP8X4),
                    rhs_scale=x_scales[:, toks],
                    start=True,
                    stop=True,
                )
                nc.scalar.activation(
                    out=zb_of[g, c][:, jj, :], in_=z[:], func=ACT.Identity, bias=bias_col[:, j : j + 1], scale=1.0
                )

        def add_residual(g, c):
            if c == 0:
                y_of[g] = rows.tile([P, TG, D], F32, name="y")
                sums_of[g] = small.tile([P, TG, NC], F32, name="chunk_sums")
            cols = slice(c * BANK, (c + 1) * BANK)
            for i in range(TG):
                zbt = psum_t.tile([P, BANK], F32, name="zbt", tag="tok")
                for jj in range(F_PER_CHUNK):
                    nc.tensor.transpose(zbt[:, jj * P : (jj + 1) * P], zb_of[g, c][:, jj, i * P : (i + 1) * P], ident_f[:])
                nc.vector.scalar_tensor_tensor(
                    out=y_of[g][:, i, cols],
                    in0=zbt[:],
                    scalar=0.0,
                    in1=r_sb[:, g * TG + i, cols],
                    op0=ALU.add,
                    op1=ALU.add,
                    accum_out=sums_of[g][:, i, c : c + 1],
                )
            if c == NC - 1:
                row_sum = small.tile([P, TG], F32, name="row_sum")
                nc.vector.tensor_reduce(out=row_sum[:], in_=sums_of[g][:], axis=AX.X, op=ALU.add)
                neg_mean_of[g] = small.tile([P, TG], F32, name="neg_mean")
                nc.vector.tensor_scalar_mul(out=neg_mean_of[g][:], in0=row_sum[:], scalar1=-1.0 / D)

        def normalise(g, i):
            neg_mean = neg_mean_of[g][:, i : i + 1]
            squares = work.tile([P, D], BF16, name="squares")
            sq_sum = small.tile([P, 1], F32, name="sq_sum")
            nc.scalar.activation(
                out=squares[:], in_=y_of[g][:, i, :], func=ACT.Square, bias=neg_mean, scale=1.0, accum_out=sq_sum[:]
            )
            std = small.tile([P, 1], F32, name="std")
            nc.scalar.activation(out=std[:], in_=sq_sum[:], func=ACT.Sqrt, bias=eps[:], scale=1.0 / D)
            o = work.tile([P, D], F32, name="o")
            nc.vector.scalar_tensor_tensor(
                out=o[:], in0=y_of[g][:, i, :], scalar=neg_mean, in1=gain_bc[:], op0=ALU.add, op1=ALU.mult
            )
            rstd = small.tile([P, 1], F32, name="rstd")
            nc.vector.reciprocal(out=rstd[:], in_=std[:])
            nc.vector.scalar_tensor_tensor(
                out=o[:], in0=o[:], scalar=rstd[:], in1=shift_bc[:], op0=ALU.mult, op1=ALU.add
            )
            nc.sync.dma_start(out=out_view[:, g * TG + i, :], in_=o[:])

        quantise_x(0)
        bias_ps = psum_t.tile([P, P], BF16, tag="tok")
        nc.tensor.transpose(bias_ps[:], bias_rows[:], ident_b[:])
        nc.vector.tensor_copy(out=bias_col[:], in_=bias_ps[:, 0:NF])
        quantise_w(0)
        multiply(0, 0)
        for g in range(NG + 1):
            for c in range(NC):
                if g == 0 and c + 1 < NC:
                    quantise_w(c + 1)
                if g + 1 < NG and c == 0:
                    quantise_x(g + 1)
                if c + 1 < NC and g < NG:
                    multiply(g, c + 1)
                if c + 1 == NC and g + 1 < NG:
                    multiply(g + 1, 0)
                if g < NG:
                    add_residual(g, c)
                if g >= 1:
                    normalise(g - 1, c)
